import numpy as np
import ml_dtypes


def mxq(x, axis, fmt="e4m3"):
    dtype, down = {"e4m3": (ml_dtypes.float8_e4m3fn, 7), "e5m2": (ml_dtypes.float8_e5m2, 14)}[fmt]
    v = np.moveaxis(np.asarray(x, np.float32).astype(ml_dtypes.bfloat16).astype(np.float64), axis, -1)
    blocks = v.reshape(v.shape[:-1] + (-1, 32))
    amax = np.abs(blocks).max(-1, keepdims=True)
    byte = np.maximum(np.where(amax > 0, np.frexp(amax)[1] - 1 + 127, 0) - down, 1)
    scale = np.exp2(byte - 127.0)
    codes = (blocks / scale).astype(np.float32).astype(dtype).astype(np.float64)
    return np.moveaxis((codes * scale).reshape(v.shape), -1, axis)


WIDE = False


def mx_kscale(k):
    if not WIDE:
        return np.ones(k)
    levels = np.array([10, -10, 5, -5, 0])
    a = np.random.permutation(np.resize(levels, k // 512 * 4)).reshape(k // 512, 4)
    idx = np.arange(k)
    return np.exp2(a[idx // 512, idx % 128 // 32])


BF16 = ml_dtypes.bfloat16


def bf(x):
    return np.asarray(x, np.float32).astype(BF16)


def f64(x):
    return np.asarray(x).astype(np.float64)


E2M1 = np.array([0.0, 0.5, 1.0, 1.5, 2.0, 3.0, 4.0, 6.0, -0.0, -0.5, -1.0, -1.5, -2.0, -3.0, -4.0, -6.0])


def pack_weight(w, fmt):
    k, n = w.shape
    w = f64(bf(w)).reshape(k // 32, 32, n)
    amax = np.abs(w).max(1)
    if fmt == "e4m3":
        byte = np.frexp(amax)[1] - 1 + 127 - 7
    else:
        mant, ex = np.frexp(amax / 6.0)
        byte = np.where(mant > 0.5, ex, ex - 1) + 127
    byte = np.clip(np.where(amax > 0, byte, 1), 1, 254)
    scaled = (w * np.exp2(127.0 - byte)[:, None, :]).reshape(k, n).astype(np.float32)
    by_word = np.ascontiguousarray(scaled.reshape(k // 512, 128, 4, n).transpose(0, 1, 3, 2))
    if fmt == "e4m3":
        words = by_word.astype(ml_dtypes.float8_e4m3fn).view(np.uint8)
    else:
        c = by_word.astype(ml_dtypes.float4_e2m1fn).view(np.uint8) & 0xF
        words = c[..., 0::2] | (c[..., 1::2] << 4)
    return np.ascontiguousarray(words), np.ascontiguousarray(byte.astype(np.uint8).reshape(k // 512, 16, n))


def unpack_weight(words, scales, fmt):
    g, p, n, _ = words.shape
    if fmt == "e4m3":
        vals = np.ascontiguousarray(words).view(ml_dtypes.float8_e4m3fn).astype(np.float64)
    else:
        nib = np.empty((g, p, n, 4), np.uint8)
        nib[..., 0::2] = words & 0xF
        nib[..., 1::2] = words >> 4
        vals = E2M1[nib]
    vals = vals * np.repeat(np.exp2(scales.astype(np.float64) - 127.0), 8, axis=1)[..., None]
    return vals.transpose(0, 1, 3, 2).reshape(g * 512, n)


B, TW, C, MS, RED = 2, 128, 512, 5, 1
T = TW * MS
D = C * MS
F = D * RED


def sigmoid(v):
    return 1.0 / (1.0 + np.exp(-v))


def setup_inputs():
    t = mx_kscale(F)
    x = bf(np.random.standard_normal((B, T, C)))
    w1_words, w1_scales = pack_weight(np.random.standard_normal((D, F)) / np.sqrt(D) * t, "e4m3")
    w2_words, w2_scales = pack_weight(np.random.standard_normal((F, D)) * 3.0 / np.sqrt(F) / t[:, None], "e4m3")
    return {"x": x,
            "w1_words": w1_words, "w1_scales": w1_scales,
            "w2_words": w2_words, "w2_scales": w2_scales}


def reference(x, w1_words, w1_scales, w2_words, w2_scales):
    xt = f64(x).reshape(B, TW, MS, C).swapaxes(-1, -2)
    flat = xt.reshape(B, TW, D)
    h = np.maximum(mxq(flat, 2, "e4m3") @ unpack_weight(w1_words, w1_scales, "e4m3"), 0.0)
    a = mxq(h, 2, "e4m3") @ unpack_weight(w2_words, w2_scales, "e4m3")
    g = sigmoid(a).reshape(B, TW, C, MS)
    e = np.exp(g - g.max(-1, keepdims=True))
    y = e / e.sum(-1, keepdims=True)
    return (xt * y).sum(-1)

@@ -1,0 +1,223 @@
+from contextlib import ExitStack
+
+import concourse.mybir as mybir
+from concourse.masks import make_identity
+
+F32 = mybir.dt.float32
+BF16 = mybir.dt.bfloat16
+I32 = mybir.dt.int32
+U32 = mybir.dt.uint32
+U8 = mybir.dt.uint8
+FP8X4 = mybir.dt.float8_e4m3fn_x4
+ACT = mybir.ActivationFunctionType
+ALU = mybir.AluOpType
+AXIS = mybir.AxisListType
+
+P = 128
+BATCH = 2
+WIN = 5
+CH = 512
+D = CH * WIN
+TOK = BATCH * P
+K_PASS = 512
+PASSES = D // K_PASS
+N_TILE = 512
+N_TILES = D // N_TILE
+SORT_CUT = 336
+MAX_RANGE = N_TILE // WIN + 1
+
+FLOPS = 2 * 2 * TOK * D * D
+
+
+def tile_dwamformer_pa_kernel(tc, x, w1_words, w1_scales, w2_words, w2_scales, out):
+    nc = tc.nc
+    with ExitStack() as ctx:
+        keep = ctx.enter_context(tc.tile_pool(name="keep", bufs=1))
+        work = ctx.enter_context(tc.tile_pool(name="work", bufs=3))
+        banks = ctx.enter_context(tc.psum_pool(name="banks", bufs=8))
+        ctx.enter_context(tc.manual_schedule())
+
+        ident = keep.tile([P, P], F32)
+        warm = keep.tile([P, 2], F32)
+        x_raw = keep.tile([P, BATCH, WIN, CH], BF16)
+        flat = keep.tile([P, BATCH, D], BF16)
+        flat_cm = flat[:].rearrange("p b (c m) -> p b c m", m=WIN)
+        w1_sb = keep.tile([P, PASSES, D], U32, align_bytes=64)
+        w2_sb = keep.tile([P, PASSES, D], U32, align_bytes=64)
+        w_sb = (w1_sb, w2_sb)
+        w_planes = keep.tile([P, 3, D], U8, align_bytes=64)
+        flat_codes = keep.tile([P, PASSES, TOK], U32, align_bytes=64)
+        flat_planes = keep.tile([P, PASSES, TOK], U8, align_bytes=64)
+        h_codes = keep.tile([P, PASSES, TOK], U32, align_bytes=64)
+        h_planes = keep.tile([P, PASSES, TOK], U8, align_bytes=64)
+        e_all = keep.tile([P, BATCH, D], F32)
+        e_cm = e_all[:].rearrange("p b (c m) -> p b c m", m=WIN)
+        out_sb = keep.tile([P, BATCH, CH], F32)
+
+        def weight_plane(which, g, cols):
+            if g < 4:
+                return w_planes[4 * g : P, which, cols]
+            return w_planes[4 * which : P, 2, cols]
+
+        nc.vector.memset(warm[:], 0.0)
+        nc.vector.memset(w_planes[:].rearrange("p s n -> p (s n)").bitcast(I32), 0)
+        nc.scalar.activation(out=warm[:, 1:2], in_=warm[:, 0:1], func=ACT.Tanh)
+        make_identity(nc, ident[:])
+
+        for b in range(BATCH):
+            nc.sync.dma_start(out=x_raw[:, b], in_=x[b].rearrange("(w m) c -> w m c", m=WIN))
+        for which, scales in enumerate((w1_scales, w2_scales)):
+            for quad in range(4):
+                rows = slice(4 * quad, 4 * quad + 4)
+                nc.sync.dma_start(
+                    out=w_planes[32 * quad : 32 * quad + 16, which, :].bitcast(I32),
+                    in_=scales[0:4, rows, :].bitcast(I32),
+                )
+                first = 32 * quad + 4 * which
+                nc.sync.dma_start(
+                    out=w_planes[first : first + 4, 2, :].bitcast(I32),
+                    in_=scales[4, rows, :].bitcast(I32),
+                )
+        for which, words in enumerate((w1_words, w2_words)):
+            for j in range(N_TILES):
+                cols = slice(j * N_TILE, (j + 1) * N_TILE)
+                for g in range(PASSES):
+                    nc.sync.dma_start(
+                        out=w_sb[which][:, g, cols].bitcast(I32),
+                        in_=words[g, :, cols, :].rearrange("p n t -> p (n t)").bitcast(I32),
+                    )
+
+        def turn(word_columns):
+            turned = banks.tile([P, BATCH, 2, P], F32, name="turned", tag="bank")
+            for b in range(BATCH):
+                for u in range(2):
+                    nc.tensor.transpose(turned[:, b, u, :], word_columns(b, u), ident[:])
+            return turned
+
+        def regroup(turned, copy):
+            grouped = work.tile([P, TOK * 4], BF16, align_bytes=64, name="grouped")
+            copy(
+                out=grouped[:].bitcast(F32).rearrange("p (b r u) -> p b r u", b=BATCH, u=2),
+                in_=turned[:].rearrange("p b u r -> p b r u"),
+            )
+            return grouped
+
+        def quantise(grouped, codes, planes, g):
+            nc.vector.quantize_mx(
+                out=codes[:, g, :].bitcast(FP8X4), scales=planes[:, g, :], in_=grouped[:]
+            )
+
+        def mx_passes(acc, codes, planes, b, which, cols, passes):
+            toks = slice(b * P, (b + 1) * P)
+            for g in passes:
+                nc.tensor.matmul_mx(
+                    out=acc,
+                    lhsT=codes[:, g, toks].bitcast(FP8X4),
+                    lhsT_scale=planes[:, g, toks],
+                    rhs=w_sb[which][:, g, cols].bitcast(FP8X4),
+                    rhs_scale=weight_plane(which, g, cols),
+                    start=(g == 0),
+                    stop=(g == PASSES - 1),
+                )
+
+        for b in range(BATCH):
+            nc.vector.tensor_copy(
+                out=flat_cm[:, b, 0:SORT_CUT, :],
+                in_=x_raw[:, b, :, 0:SORT_CUT].rearrange("p m c -> p c m"),
+            )
+            nc.scalar.copy(
+                out=flat_cm[:, b, SORT_CUT:CH, :],
+                in_=x_raw[:, b, :, SORT_CUT:CH].rearrange("p m c -> p c m"),
+            )
+
+        def flat_words(g):
+            def columns(b, u):
+                words = flat[:, b, :].bitcast(F32)
+                return words[:, 256 * g + u : 256 * (g + 1) : 2]
+
+            return columns
+
+        turned_flat = [turn(flat_words(g)) for g in range(PASSES)]
+        grouped_flat = []
+        for g in range(PASSES):
+            copy = nc.scalar.copy if g % 2 == 0 else nc.vector.tensor_copy
+            grouped_flat.append(regroup(turned_flat[g], copy))
+            if g > 0:
+                quantise(grouped_flat[g - 1], flat_codes, flat_planes, g - 1)
+        quantise(grouped_flat[PASSES - 1], flat_codes, flat_planes, PASSES - 1)
+
+        def pack_h(h_sorted, g):
+            def columns(b, u):
+                return h_sorted[:, b, :].bitcast(F32)[:, u * P : (u + 1) * P]
+
+            grouped = regroup(turn(columns), nc.vector.tensor_copy)
+            quantise(grouped, h_codes, h_planes, g)
+
+        h_tiles = []
+        for j in range(N_TILES):
+            h_sorted = work.tile([P, BATCH, K_PASS], BF16, name="h_sorted")
+            h_tiles.append(h_sorted)
+            for b in range(BATCH):
+                acc = banks.tile([P, N_TILE], F32, name="acc", tag="bank")
+                cols = slice(j * N_TILE, (j + 1) * N_TILE)
+                mx_passes(acc[:], flat_codes, flat_planes, b, 0, cols, range(PASSES))
+                nc.scalar.activation(
+                    out=h_sorted[:, b, :].rearrange("q (u p e) -> q u p e", u=2, e=2),
+                    in_=acc[:].rearrange("q (p u e) -> q u p e", u=2, e=2),
+                    func=ACT.Relu,
+                )
+                if b == 0 and j > 0:
+                    pack_h(h_tiles[j - 1], j - 1)
+
+        tiles = [(0, 128), (128, 128), (256, 256)] + [(j * N_TILE, N_TILE) for j in range(1, N_TILES)]
+        head = 3
+        opened = {}
+        for i in range(head):
+            start, width = tiles[i]
+            for b in range(BATCH):
+                acc = banks.tile([P, N_TILE], F32, name="acc", tag="bank")
+                opened[(i, b)] = acc
+                mx_passes(acc[:, 0:width], h_codes, h_planes, b, 1, slice(start, start + width), range(PASSES - 1))
+            if i == 0:
+                pack_h(h_tiles[N_TILES - 1], N_TILES - 1)
+
+        def finish(c0, c1, num, rden):
+            n = c1 - c0
+            nc.gpsimd.tensor_tensor(
+                out=out_sb[:, :, c0:c1], in0=num[:, :, 0:n], in1=rden[:, :, 0:n], op=ALU.mult
+            )
+
+        waiting = None
+        for i in range(len(tiles)):
+            start, width = tiles[i]
+            cols = slice(start, start + width)
+            th = work.tile([P, BATCH, N_TILE], F32, name="th")
+            for b in range(BATCH):
+                if i < head:
+                    acc = opened[(i, b)]
+                    mx_passes(acc[:, 0:width], h_codes, h_planes, b, 1, cols, range(PASSES - 1, PASSES))
+                else:
+                    acc = banks.tile([P, N_TILE], F32, name="acc", tag="bank")
+                    mx_passes(acc[:, 0:width], h_codes, h_planes, b, 1, cols, range(PASSES))
+                nc.scalar.activation(out=th[:, b, 0:width], in_=acc[:, 0:width], func=ACT.Tanh, scale=0.5)
+            nc.scalar.activation(out=e_all[:, :, cols], in_=th[:, :, 0:width], func=ACT.Exp, scale=0.5)
+
+            c0 = start // WIN
+            c1 = (start + width) // WIN
+            n = c1 - c0
+            xe = work.tile([P, BATCH, MAX_RANGE, WIN], F32, name="xe")
+            den = work.tile([P, BATCH, MAX_RANGE], F32, name="den")
+            rden = work.tile([P, BATCH, MAX_RANGE], F32, name="rden")
+            num = work.tile([P, BATCH, MAX_RANGE], F32, name="num")
+            nc.gpsimd.tensor_tensor(
+                out=xe[:, :, 0:n, :], in0=e_cm[:, :, c0:c1, :], in1=flat_cm[:, :, c0:c1, :], op=ALU.mult
+            )
+            if waiting is not None:
+                finish(*waiting)
+            nc.vector.tensor_reduce(out=den[:, :, 0:n], in_=e_cm[:, :, c0:c1, :], axis=AXIS.X, op=ALU.add)
+            nc.vector.reciprocal(out=rden[:, :, 0:n], in_=den[:, :, 0:n])
+            nc.vector.tensor_reduce(out=num[:, :, 0:n], in_=xe[:, :, 0:n, :], axis=AXIS.X, op=ALU.add)
+            waiting = (c0, c1, num, rden)
+        finish(*waiting)
+
+        nc.sync.dma_start(out=out.rearrange("b w c -> w b c"), in_=out_sb[:])

@@ -24,7 +24,9 @@ PASSES = D // K_PASS
 N_TILE = 512
 N_TILES = D // N_TILE
 SORT_CUT = 336
-MAX_RANGE = N_TILE // WIN + 1
+SUPER = P * WIN
+SUPERS = D // SUPER
+REST = SUPER - N_TILE
 
 FLOPS = 2 * 2 * TOK * D * D
 
@@ -34,6 +36,7 @@ def tile_dwamformer_pa_kernel(tc, x, w1_words, w1_scales, w2_words, w2_scales, o
     with ExitStack() as ctx:
         keep = ctx.enter_context(tc.tile_pool(name="keep", bufs=1))
         work = ctx.enter_context(tc.tile_pool(name="work", bufs=3))
+        gate = ctx.enter_context(tc.tile_pool(name="gate", bufs=4))
         banks = ctx.enter_context(tc.psum_pool(name="banks", bufs=8))
         ctx.enter_context(tc.manual_schedule())
 
@@ -50,9 +53,6 @@ def tile_dwamformer_pa_kernel(tc, x, w1_words, w1_scales, w2_words, w2_scales, o
         flat_planes = keep.tile([P, PASSES, TOK], U8, align_bytes=64)
         h_codes = keep.tile([P, PASSES, TOK], U32, align_bytes=64)
         h_planes = keep.tile([P, PASSES, TOK], U8, align_bytes=64)
-        e_all = keep.tile([P, BATCH, D], F32)
-        e_cm = e_all[:].rearrange("p b (c m) -> p b c m", m=WIN)
-        out_sb = keep.tile([P, BATCH, CH], F32)
 
         def weight_plane(which, g, cols):
             if g < 4:
@@ -78,9 +78,9 @@ def tile_dwamformer_pa_kernel(tc, x, w1_words, w1_scales, w2_words, w2_scales, o
                     out=w_planes[first : first + 4, 2, :].bitcast(I32),
                     in_=scales[4, rows, :].bitcast(I32),
                 )
-        for which, words in enumerate((w1_words, w2_words)):
-            for j in range(N_TILES):
-                cols = slice(j * N_TILE, (j + 1) * N_TILE)
+        for which, words, width in ((0, w1_words, N_TILE), (1, w2_words, SUPER)):
+            for j in range(D // width):
+                cols = slice(j * width, (j + 1) * width)
                 for g in range(PASSES):
                     nc.sync.dma_start(
                         out=w_sb[which][:, g, cols].bitcast(I32),
@@ -169,55 +169,73 @@ def tile_dwamformer_pa_kernel(tc, x, w1_words, w1_scales, w2_words, w2_scales, o
                 if b == 0 and j > 0:
                     pack_h(h_tiles[j - 1], j - 1)
 
-        tiles = [(0, 128), (128, 128), (256, 256)] + [(j * N_TILE, N_TILE) for j in range(1, N_TILES)]
-        head = 3
-        opened = {}
-        for i in range(head):
-            start, width = tiles[i]
-            for b in range(BATCH):
-                acc = banks.tile([P, N_TILE], F32, name="acc", tag="bank")
-                opened[(i, b)] = acc
-                mx_passes(acc[:, 0:width], h_codes, h_planes, b, 1, slice(start, start + width), range(PASSES - 1))
-            if i == 0:
+        def gate_banks():
+            wide = banks.tile([P, N_TILE], F32, name="wide", tag="bank")
+            narrow = banks.tile([P, N_TILE], F32, name="narrow", tag="bank")
+            return wide, narrow
+
+        def gate_passes(wide, narrow, k, b, passes):
+            first = k * SUPER
+            mx_passes(wide[:], h_codes, h_planes, b, 1, slice(first, first + N_TILE), passes)
+            mx_passes(narrow[:, 0:REST], h_codes, h_planes, b, 1, slice(first + N_TILE, first + SUPER), passes)
+
+        opened = []
+        for b in range(BATCH):
+            opened.append(gate_banks())
+            gate_passes(opened[b][0], opened[b][1], 0, b, range(PASSES - 1))
+            if b == 0:
                 pack_h(h_tiles[N_TILES - 1], N_TILES - 1)
 
-        def finish(c0, c1, num, rden):
-            n = c1 - c0
+        def finish(k, sums_x, sums_other, r_both):
+            chans = slice(k * P, (k + 1) * P)
+            cross = gate.tile([P, BATCH, P], F32, name="cross")
+            pooled = gate.tile([P, BATCH, P], F32, name="pooled")
+            nc.gpsimd.tensor_tensor(out=cross[:], in0=sums_x[:], in1=sums_other[:], op=ALU.mult)
             nc.gpsimd.tensor_tensor(
-                out=out_sb[:, :, c0:c1], in0=num[:, :, 0:n], in1=rden[:, :, 0:n], op=ALU.mult
+                out=pooled[:], in0=cross[:], in1=r_both[:].unsqueeze(1).to_broadcast([P, BATCH, P]), op=ALU.mult
             )
+            nc.sync.dma_start(out=out[:, :, chans].rearrange("b w c -> w b c"), in_=pooled[:])
 
         waiting = None
-        for i in range(len(tiles)):
-            start, width = tiles[i]
-            cols = slice(start, start + width)
-            th = work.tile([P, BATCH, N_TILE], F32, name="th")
+        for k in range(SUPERS):
+            sums_x = gate.tile([P, BATCH, P], F32, name="sums_x")
+            sums_other = gate.tile([P, BATCH, P], F32, name="sums_other")
+            den_both = gate.tile([P, P], F32, name="den_both")
+            r_both = gate.tile([P, P], F32, name="r_both")
+            weighted = []
             for b in range(BATCH):
-                if i < head:
-                    acc = opened[(i, b)]
-                    mx_passes(acc[:, 0:width], h_codes, h_planes, b, 1, cols, range(PASSES - 1, PASSES))
+                if k == 0:
+                    wide, narrow = opened[b]
+                    gate_passes(wide, narrow, k, b, range(PASSES - 1, PASSES))
                 else:
-                    acc = banks.tile([P, N_TILE], F32, name="acc", tag="bank")
-                    mx_passes(acc[:, 0:width], h_codes, h_planes, b, 1, cols, range(PASSES))
-                nc.scalar.activation(out=th[:, b, 0:width], in_=acc[:, 0:width], func=ACT.Tanh, scale=0.5)
-            nc.scalar.activation(out=e_all[:, :, cols], in_=th[:, :, 0:width], func=ACT.Exp, scale=0.5)
-
-            c0 = start // WIN
-            c1 = (start + width) // WIN
-            n = c1 - c0
-            xe = work.tile([P, BATCH, MAX_RANGE, WIN], F32, name="xe")
-            den = work.tile([P, BATCH, MAX_RANGE], F32, name="den")
-            rden = work.tile([P, BATCH, MAX_RANGE], F32, name="rden")
-            num = work.tile([P, BATCH, MAX_RANGE], F32, name="num")
-            nc.gpsimd.tensor_tensor(
-                out=xe[:, :, 0:n, :], in0=e_cm[:, :, c0:c1, :], in1=flat_cm[:, :, c0:c1, :], op=ALU.mult
-            )
+                    wide, narrow = gate_banks()
+                    gate_passes(wide, narrow, k, b, range(PASSES))
+                th = gate.tile([P, SUPER], F32, name="th")
+                e = gate.tile([P, SUPER], F32, name="e")
+                xe = gate.tile([P, SUPER], F32, name="xe")
+                weighted.append(xe)
+                nc.scalar.activation(out=th[:, 0:N_TILE], in_=wide[:], func=ACT.Tanh, scale=0.5)
+                nc.scalar.activation(out=th[:, N_TILE:SUPER], in_=narrow[:, 0:REST], func=ACT.Tanh, scale=0.5)
+                nc.scalar.activation(out=e[:], in_=th[:], func=ACT.Exp, scale=0.5)
+                nc.gpsimd.tensor_tensor(
+                    out=xe[:], in0=e[:], in1=flat[:, b, k * SUPER : (k + 1) * SUPER], op=ALU.mult
+                )
+                nc.vector.tensor_reduce(
+                    out=sums_other[:, 1 - b, :],
+                    in_=e[:].rearrange("p (c m) -> p c m", m=WIN),
+                    axis=AXIS.X,
+                    op=ALU.add,
+                )
             if waiting is not None:
                 finish(*waiting)
-            nc.vector.tensor_reduce(out=den[:, :, 0:n], in_=e_cm[:, :, c0:c1, :], axis=AXIS.X, op=ALU.add)
-            nc.vector.reciprocal(out=rden[:, :, 0:n], in_=den[:, :, 0:n])
-            nc.vector.tensor_reduce(out=num[:, :, 0:n], in_=xe[:, :, 0:n, :], axis=AXIS.X, op=ALU.add)
-            waiting = (c0, c1, num, rden)
+            nc.vector.tensor_tensor(out=den_both[:], in0=sums_other[:, 0, :], in1=sums_other[:, 1, :], op=ALU.mult)
+            nc.vector.reciprocal(out=r_both[:], in_=den_both[:])
+            for b in range(BATCH):
+                nc.vector.tensor_reduce(
+                    out=sums_x[:, b, :],
+                    in_=weighted[b][:].rearrange("p (c m) -> p c m", m=WIN),
+                    axis=AXIS.X,
+                    op=ALU.add,
+                )
+            waiting = (k, sums_x, sums_other, r_both)
         finish(*waiting)
-
-        nc.sync.dma_start(out=out.rearrange("b w c -> w b c"), in_=out_sb[:])

@@ -49,10 +49,10 @@ def tile_dwamformer_pa_kernel(tc, x, w1_words, w1_scales, w2_words, w2_scales, o
         w2_sb = keep.tile([P, PASSES, D], U32, align_bytes=64)
         w_sb = (w1_sb, w2_sb)
         w_planes = keep.tile([P, 3, D], U8, align_bytes=64)
-        flat_codes = keep.tile([P, PASSES, TOK], U32, align_bytes=64)
-        flat_planes = keep.tile([P, PASSES, TOK], U8, align_bytes=64)
-        h_codes = keep.tile([P, PASSES, TOK], U32, align_bytes=64)
-        h_planes = keep.tile([P, PASSES, TOK], U8, align_bytes=64)
+        flat_codes = keep.tile([P, BATCH, PASSES, P], U32, align_bytes=64)
+        flat_planes = keep.tile([P, BATCH, PASSES, P], U8, align_bytes=64)
+        h_codes = keep.tile([P, PASSES, BATCH, P], U32, align_bytes=64)
+        h_planes = keep.tile([P, PASSES, BATCH, P], U8, align_bytes=64)
 
         def weight_plane(which, g, cols):
             if g < 4:
@@ -64,20 +64,23 @@ def tile_dwamformer_pa_kernel(tc, x, w1_words, w1_scales, w2_words, w2_scales, o
         nc.scalar.activation(out=warm[:, 1:2], in_=warm[:, 0:1], func=ACT.Tanh)
         make_identity(nc, ident[:])
 
-        for b in range(BATCH):
-            nc.sync.dma_start(out=x_raw[:, b], in_=x[b].rearrange("(w m) c -> w m c", m=WIN))
-        for which, scales in enumerate((w1_scales, w2_scales)):
+        def load_planes(queue, view, which, scales):
             for quad in range(4):
                 rows = slice(4 * quad, 4 * quad + 4)
-                nc.sync.dma_start(
-                    out=w_planes[32 * quad : 32 * quad + 16, which, :].bitcast(I32),
-                    in_=scales[0:4, rows, :].bitcast(I32),
+                queue.dma_start(
+                    out=w_planes[32 * quad : 32 * quad + 16, which, :].bitcast(view),
+                    in_=scales[0:4, rows, :].bitcast(view),
                 )
                 first = 32 * quad + 4 * which
-                nc.sync.dma_start(
-                    out=w_planes[first : first + 4, 2, :].bitcast(I32),
-                    in_=scales[4, rows, :].bitcast(I32),
+                queue.dma_start(
+                    out=w_planes[first : first + 4, 2, :].bitcast(view),
+                    in_=scales[4, rows, :].bitcast(view),
                 )
+
+        for b in range(BATCH):
+            nc.sync.dma_start(out=x_raw[:, b], in_=x[b].rearrange("(w m) c -> w m c", m=WIN))
+        load_planes(nc.sync, I32, 0, w1_scales)
+        load_planes(nc.sync, I32, 1, w2_scales)
         for which, words, width in ((0, w1_words, N_TILE), (1, w2_words, SUPER)):
             for j in range(D // width):
                 cols = slice(j * width, (j + 1) * width)
@@ -87,33 +90,34 @@ def tile_dwamformer_pa_kernel(tc, x, w1_words, w1_scales, w2_words, w2_scales, o
                         in_=words[g, :, cols, :].rearrange("p n t -> p (n t)").bitcast(I32),
                     )
 
-        def turn(word_columns):
-            turned = banks.tile([P, BATCH, 2, P], F32, name="turned", tag="bank")
-            for b in range(BATCH):
+        def turn(sources):
+            turned = banks.tile([P, 2, 2, P], F32, name="turned", tag="bank")
+            for s in range(len(sources)):
                 for u in range(2):
-                    nc.tensor.transpose(turned[:, b, u, :], word_columns(b, u), ident[:])
+                    nc.tensor.transpose(turned[:, s, u, :], sources[s][:, u, :], ident[:])
             return turned
 
-        def regroup(turned, copy):
-            grouped = work.tile([P, TOK * 4], BF16, align_bytes=64, name="grouped")
+        def regroup(turned, n, copy):
+            grouped = work.tile([P, 2 * K_PASS], BF16, align_bytes=64, name="grouped")
             copy(
-                out=grouped[:].bitcast(F32).rearrange("p (b r u) -> p b r u", b=BATCH, u=2),
-                in_=turned[:].rearrange("p b u r -> p b r u"),
+                out=grouped[:, 0 : n * K_PASS].bitcast(F32).rearrange("p (s r u) -> p s r u", s=n, u=2),
+                in_=turned[:, 0:n].rearrange("p s u r -> p s r u"),
             )
             return grouped
 
-        def quantise(grouped, codes, planes, g):
+        def quantise(grouped, n, codes, planes):
             nc.vector.quantize_mx(
-                out=codes[:, g, :].bitcast(FP8X4), scales=planes[:, g, :], in_=grouped[:]
+                out=codes.rearrange("p s r -> p (s r)").bitcast(FP8X4),
+                scales=planes.rearrange("p s r -> p (s r)"),
+                in_=grouped[:, 0 : n * K_PASS],
             )
 
-        def mx_passes(acc, codes, planes, b, which, cols, passes):
-            toks = slice(b * P, (b + 1) * P)
-            for g in passes:
+        def mx_group(acc, codes_of, planes_of, which, cols):
+            for g in range(PASSES):
                 nc.tensor.matmul_mx(
                     out=acc,
-                    lhsT=codes[:, g, toks].bitcast(FP8X4),
-                    lhsT_scale=planes[:, g, toks],
+                    lhsT=codes_of(g).bitcast(FP8X4),
+                    lhsT_scale=planes_of(g),
                     rhs=w_sb[which][:, g, cols].bitcast(FP8X4),
                     rhs_scale=weight_plane(which, g, cols),
                     start=(g == 0),
@@ -130,28 +134,25 @@ def tile_dwamformer_pa_kernel(tc, x, w1_words, w1_scales, w2_words, w2_scales, o
                 in_=x_raw[:, b, :, SORT_CUT:CH].rearrange("p m c -> p c m"),
             )
 
-        def flat_words(g):
-            def columns(b, u):
-                words = flat[:, b, :].bitcast(F32)
-                return words[:, 256 * g + u : 256 * (g + 1) : 2]
+        def flat_words(b, g):
+            words = flat[:, b, g * K_PASS : (g + 1) * K_PASS].bitcast(F32)
+            return words.rearrange("q (p u) -> q u p", u=2)
 
-            return columns
-
-        turned_flat = [turn(flat_words(g)) for g in range(PASSES)]
+        packs = [(b, g, min(2, PASSES - g)) for b in range(BATCH) for g in range(0, PASSES, 2)]
+        turned_flat = [turn([flat_words(b, g + s) for s in range(n)]) for b, g, n in packs]
         grouped_flat = []
-        for g in range(PASSES):
-            copy = nc.scalar.copy if g % 2 == 0 else nc.vector.tensor_copy
-            grouped_flat.append(regroup(turned_flat[g], copy))
-            if g > 0:
-                quantise(grouped_flat[g - 1], flat_codes, flat_planes, g - 1)
-        quantise(grouped_flat[PASSES - 1], flat_codes, flat_planes, PASSES - 1)
+        for i in range(len(packs) + 1):
+            if i < len(packs):
+                copy = nc.scalar.copy if i % 2 == 0 else nc.vector.tensor_copy
+                grouped_flat.append(regroup(turned_flat[i], packs[i][2], copy))
+            if i > 0:
+                b, g, n = packs[i - 1]
+                quantise(grouped_flat[i - 1], n, flat_codes[:, b, g : g + n, :], flat_planes[:, b, g : g + n, :])
 
         def pack_h(h_sorted, g):
-            def columns(b, u):
-                return h_sorted[:, b, :].bitcast(F32)[:, u * P : (u + 1) * P]
-
-            grouped = regroup(turn(columns), nc.vector.tensor_copy)
-            quantise(grouped, h_codes, h_planes, g)
+            sources = [h_sorted[:, b, :].bitcast(F32).rearrange("q (u p) -> q u p", u=2) for b in range(BATCH)]
+            grouped = regroup(turn(sources), BATCH, nc.vector.tensor_copy)
+            quantise(grouped, BATCH, h_codes[:, g], h_planes[:, g])
 
         h_tiles = []
         for j in range(N_TILES):
@@ -159,8 +160,13 @@ def tile_dwamformer_pa_kernel(tc, x, w1_words, w1_scales, w2_words, w2_scales, o
             h_tiles.append(h_sorted)
             for b in range(BATCH):
                 acc = banks.tile([P, N_TILE], F32, name="acc", tag="bank")
-                cols = slice(j * N_TILE, (j + 1) * N_TILE)
-                mx_passes(acc[:], flat_codes, flat_planes, b, 0, cols, range(PASSES))
+                mx_group(
+                    acc[:],
+                    lambda g: flat_codes[:, b, g, :],
+                    lambda g: flat_planes[:, b, g, :],
+                    0,
+                    slice(j * N_TILE, (j + 1) * N_TILE),
+                )
                 nc.scalar.activation(
                     out=h_sorted[:, b, :].rearrange("q (u p e) -> q u p e", u=2, e=2),
                     in_=acc[:].rearrange("q (p u e) -> q u p e", u=2, e=2),
@@ -168,74 +174,41 @@ def tile_dwamformer_pa_kernel(tc, x, w1_words, w1_scales, w2_words, w2_scales, o
                 )
                 if b == 0 and j > 0:
                     pack_h(h_tiles[j - 1], j - 1)
+        pack_h(h_tiles[N_TILES - 1], N_TILES - 1)
 
-        def gate_banks():
-            wide = banks.tile([P, N_TILE], F32, name="wide", tag="bank")
-            narrow = banks.tile([P, N_TILE], F32, name="narrow", tag="bank")
-            return wide, narrow
-
-        def gate_passes(wide, narrow, k, b, passes):
-            first = k * SUPER
-            mx_passes(wide[:], h_codes, h_planes, b, 1, slice(first, first + N_TILE), passes)
-            mx_passes(narrow[:, 0:REST], h_codes, h_planes, b, 1, slice(first + N_TILE, first + SUPER), passes)
-
-        opened = []
-        for b in range(BATCH):
-            opened.append(gate_banks())
-            gate_passes(opened[b][0], opened[b][1], 0, b, range(PASSES - 1))
-            if b == 0:
-                pack_h(h_tiles[N_TILES - 1], N_TILES - 1)
-
-        def finish(k, sums_x, sums_other, r_both):
-            chans = slice(k * P, (k + 1) * P)
-            cross = gate.tile([P, BATCH, P], F32, name="cross")
-            pooled = gate.tile([P, BATCH, P], F32, name="pooled")
-            nc.gpsimd.tensor_tensor(out=cross[:], in0=sums_x[:], in1=sums_other[:], op=ALU.mult)
-            nc.gpsimd.tensor_tensor(
-                out=pooled[:], in0=cross[:], in1=r_both[:].unsqueeze(1).to_broadcast([P, BATCH, P]), op=ALU.mult
-            )
-            nc.sync.dma_start(out=out[:, :, chans].rearrange("b w c -> w b c"), in_=pooled[:])
-
-        waiting = None
+        den = keep.tile([P, BATCH, CH], F32)
+        num = keep.tile([P, BATCH, CH], F32)
         for k in range(SUPERS):
-            sums_x = gate.tile([P, BATCH, P], F32, name="sums_x")
-            sums_other = gate.tile([P, BATCH, P], F32, name="sums_other")
-            den_both = gate.tile([P, P], F32, name="den_both")
-            r_both = gate.tile([P, P], F32, name="r_both")
-            weighted = []
+            first = k * SUPER
+            chans = slice(k * P, (k + 1) * P)
             for b in range(BATCH):
-                if k == 0:
-                    wide, narrow = opened[b]
-                    gate_passes(wide, narrow, k, b, range(PASSES - 1, PASSES))
-                else:
-                    wide, narrow = gate_banks()
-                    gate_passes(wide, narrow, k, b, range(PASSES))
+                wide = banks.tile([P, N_TILE], F32, name="wide", tag="bank")
+                narrow = banks.tile([P, N_TILE], F32, name="narrow", tag="bank")
+                for acc, cols in (
+                    (wide[:], slice(first, first + N_TILE)),
+                    (narrow[:, 0:REST], slice(first + N_TILE, first + SUPER)),
+                ):
+                    mx_group(acc, lambda g: h_codes[:, g, b, :], lambda g: h_planes[:, g, b, :], 1, cols)
                 th = gate.tile([P, SUPER], F32, name="th")
                 e = gate.tile([P, SUPER], F32, name="e")
                 xe = gate.tile([P, SUPER], F32, name="xe")
-                weighted.append(xe)
                 nc.scalar.activation(out=th[:, 0:N_TILE], in_=wide[:], func=ACT.Tanh, scale=0.5)
                 nc.scalar.activation(out=th[:, N_TILE:SUPER], in_=narrow[:, 0:REST], func=ACT.Tanh, scale=0.5)
                 nc.scalar.activation(out=e[:], in_=th[:], func=ACT.Exp, scale=0.5)
-                nc.gpsimd.tensor_tensor(
-                    out=xe[:], in0=e[:], in1=flat[:, b, k * SUPER : (k + 1) * SUPER], op=ALU.mult
+                nc.gpsimd.tensor_tensor(out=xe[:], in0=e[:], in1=flat[:, b, first : first + SUPER], op=ALU.mult)
+                nc.vector.tensor_reduce(
+                    out=den[:, b, chans], in_=e[:].rearrange("p (c m) -> p c m", m=WIN), axis=AXIS.X, op=ALU.add
                 )
                 nc.vector.tensor_reduce(
-                    out=sums_other[:, 1 - b, :],
-                    in_=e[:].rearrange("p (c m) -> p c m", m=WIN),
-                    axis=AXIS.X,
-                    op=ALU.add,
+                    out=num[:, b, chans], in_=xe[:].rearrange("p (c m) -> p c m", m=WIN), axis=AXIS.X, op=ALU.add
                 )
-            if waiting is not None:
-                finish(*waiting)
-            nc.vector.tensor_tensor(out=den_both[:], in0=sums_other[:, 0, :], in1=sums_other[:, 1, :], op=ALU.mult)
-            nc.vector.reciprocal(out=r_both[:], in_=den_both[:])
-            for b in range(BATCH):
-                nc.vector.tensor_reduce(
-                    out=sums_x[:, b, :],
-                    in_=weighted[b][:].rearrange("p (c m) -> p c m", m=WIN),
-                    axis=AXIS.X,
-                    op=ALU.add,
-                )
-            waiting = (k, sums_x, sums_other, r_both)
-        finish(*waiting)
+
+        ln_den = keep.tile([P, BATCH, CH], F32)
+        r_den = keep.tile([P, BATCH, CH], F32)
+        pooled = keep.tile([P, BATCH, CH], F32)
+        for b in range(BATCH):
+            nc.scalar.activation(out=ln_den[:, b, :], in_=den[:, b, :], func=ACT.Abs_reciprocal_sqrt)
+        for b in range(BATCH):
+            nc.scalar.activation(out=r_den[:, b, :], in_=ln_den[:, b, :], func=ACT.Square)
+            nc.vector.tensor_tensor(out=pooled[:, b, :], in0=num[:, b, :], in1=r_den[:, b, :], op=ALU.mult)
+            nc.sync.dma_start(out=out[b], in_=pooled[:, b, :])

@@ -48,7 +48,7 @@ def tile_dwamformer_pa_kernel(tc, x, w1_words, w1_scales, w2_words, w2_scales, o
         w1_sb = keep.tile([P, PASSES, D], U32, align_bytes=64)
         w2_sb = keep.tile([P, PASSES, D], U32, align_bytes=64)
         w_sb = (w1_sb, w2_sb)
-        w_planes = keep.tile([P, 3, D], U8, align_bytes=64)
+        w_planes = keep.tile([P, 4, D], U8, align_bytes=64)
         flat_codes = keep.tile([P, BATCH, PASSES, P], U32, align_bytes=64)
         flat_planes = keep.tile([P, BATCH, PASSES, P], U8, align_bytes=64)
         h_codes = keep.tile([P, PASSES, BATCH, P], U32, align_bytes=64)
@@ -57,7 +57,7 @@ def tile_dwamformer_pa_kernel(tc, x, w1_words, w1_scales, w2_words, w2_scales, o
         def weight_plane(which, g, cols):
             if g < 4:
                 return w_planes[4 * g : P, which, cols]
-            return w_planes[4 * which : P, 2, cols]
+            return w_planes[:, 2 + which, cols]
 
         nc.vector.memset(warm[:], 0.0)
         nc.vector.memset(w_planes[:].rearrange("p s n -> p (s n)").bitcast(I32), 0)
@@ -71,17 +71,15 @@ def tile_dwamformer_pa_kernel(tc, x, w1_words, w1_scales, w2_words, w2_scales, o
                     out=w_planes[32 * quad : 32 * quad + 16, which, :].bitcast(view),
                     in_=scales[0:4, rows, :].bitcast(view),
                 )
-                first = 32 * quad + 4 * which
                 queue.dma_start(
-                    out=w_planes[first : first + 4, 2, :].bitcast(view),
+                    out=w_planes[32 * quad : 32 * quad + 4, 2 + which, :].bitcast(view),
                     in_=scales[4, rows, :].bitcast(view),
                 )
 
         for b in range(BATCH):
             nc.sync.dma_start(out=x_raw[:, b], in_=x[b].rearrange("(w m) c -> w m c", m=WIN))
-        load_planes(nc.sync, I32, 0, w1_scales)
-        load_planes(nc.sync, I32, 1, w2_scales)
-        for which, words, width in ((0, w1_words, N_TILE), (1, w2_words, SUPER)):
+        for which, words, scales, width in ((0, w1_words, w1_scales, N_TILE), (1, w2_words, w2_scales, SUPER)):
+            load_planes(nc.sync, I32, which, scales)
             for j in range(D // width):
                 cols = slice(j * width, (j + 1) * width)
                 for g in range(PASSES):

@@ -23,9 +23,11 @@ K_PASS = 512
 PASSES = D // K_PASS
 N_TILE = 512
 N_TILES = D // N_TILE
-SORT_CUT = 336
+SORT_RUN = 4
+SORT_CUTS = (0, 104, 208, 308, 412, 512)
 SUPER = P * WIN
 SUPERS = D // SUPER
+W1_CHUNKS = ((0, 1), (2, 3), (4,))
 REST = SUPER - N_TILE
 
 FLOPS = 2 * 2 * TOK * D * D
@@ -56,32 +58,34 @@ def tile_dwamformer_pa_kernel(tc, x, w1_words, w1_scales, w2_words, w2_scales, o
 
         def weight_plane(which, g, cols):
             if g < 4:
-                return w_planes[4 * g : P, which, cols]
-            return w_planes[:, 2 + which, cols]
+                return w_planes[4 * g : P, 2 * which, cols]
+            return w_planes[:, 2 * which + 1, cols]
 
         nc.vector.memset(warm[:], 0.0)
-        nc.vector.memset(w_planes[:].rearrange("p s n -> p (s n)").bitcast(I32), 0)
+        nc.vector.memset(w_planes[:, 0:2].rearrange("p s n -> p (s n)").bitcast(I32), 0)
         nc.scalar.activation(out=warm[:, 1:2], in_=warm[:, 0:1], func=ACT.Tanh)
         make_identity(nc, ident[:])
+        nc.gpsimd.memset(w_planes[:, 2:4].rearrange("p s n -> p (s n)").bitcast(I32), 0)
 
         def load_planes(queue, view, which, scales):
             for quad in range(4):
                 rows = slice(4 * quad, 4 * quad + 4)
                 queue.dma_start(
-                    out=w_planes[32 * quad : 32 * quad + 16, which, :].bitcast(view),
+                    out=w_planes[32 * quad : 32 * quad + 16, 2 * which, :].bitcast(view),
                     in_=scales[0:4, rows, :].bitcast(view),
                 )
                 queue.dma_start(
-                    out=w_planes[32 * quad : 32 * quad + 4, 2 + which, :].bitcast(view),
+                    out=w_planes[32 * quad : 32 * quad + 4, 2 * which + 1, :].bitcast(view),
                     in_=scales[4, rows, :].bitcast(view),
                 )
 
         for b in range(BATCH):
             nc.sync.dma_start(out=x_raw[:, b], in_=x[b].rearrange("(w m) c -> w m c", m=WIN))
-        for which, words, scales, width in ((0, w1_words, w1_scales, N_TILE), (1, w2_words, w2_scales, SUPER)):
+        w1_chunks = [slice(tiles[0] * N_TILE, (tiles[-1] + 1) * N_TILE) for tiles in W1_CHUNKS]
+        w2_chunks = [slice(k * SUPER, (k + 1) * SUPER) for k in range(SUPERS)]
+        for which, words, scales, chunks in ((0, w1_words, w1_scales, w1_chunks), (1, w2_words, w2_scales, w2_chunks)):
             load_planes(nc.sync, I32, which, scales)
-            for j in range(D // width):
-                cols = slice(j * width, (j + 1) * width)
+            for cols in chunks:
                 for g in range(PASSES):
                     nc.sync.dma_start(
                         out=w_sb[which][:, g, cols].bitcast(I32),
@@ -110,8 +114,8 @@ def tile_dwamformer_pa_kernel(tc, x, w1_words, w1_scales, w2_words, w2_scales, o
                 in_=grouped[:, 0 : n * K_PASS],
             )
 
-        def mx_group(acc, codes_of, planes_of, which, cols):
-            for g in range(PASSES):
+        def mx_passes(acc, codes_of, planes_of, which, cols, groups=range(PASSES)):
+            for g in groups:
                 nc.tensor.matmul_mx(
                     out=acc,
                     lhsT=codes_of(g).bitcast(FP8X4),
@@ -122,15 +126,18 @@ def tile_dwamformer_pa_kernel(tc, x, w1_words, w1_scales, w2_words, w2_scales, o
                     stop=(g == PASSES - 1),
                 )
 
+        def sort(copy, b, step):
+            chans = slice(SORT_CUTS[step], SORT_CUTS[step + 1])
+            copy(
+                out=flat_cm[:, b, chans, :].rearrange("p (c i) m -> p c m i", i=SORT_RUN),
+                in_=x_raw[:, b, :, chans].rearrange("p m (c i) -> p c m i", i=SORT_RUN),
+            )
+
         for b in range(BATCH):
-            nc.vector.tensor_copy(
-                out=flat_cm[:, b, 0:SORT_CUT, :],
-                in_=x_raw[:, b, :, 0:SORT_CUT].rearrange("p m c -> p c m"),
-            )
-            nc.scalar.copy(
-                out=flat_cm[:, b, SORT_CUT:CH, :],
-                in_=x_raw[:, b, :, SORT_CUT:CH].rearrange("p m c -> p c m"),
-            )
+            for step in range(3):
+                sort(nc.vector.tensor_copy, b, step)
+            for step in range(3, 5):
+                sort(nc.scalar.copy, b, step)
 
         def flat_words(b, g):
             words = flat[:, b, g * K_PASS : (g + 1) * K_PASS].bitcast(F32)
@@ -147,51 +154,85 @@ def tile_dwamformer_pa_kernel(tc, x, w1_words, w1_scales, w2_words, w2_scales, o
                 b, g, n = packs[i - 1]
                 quantise(grouped_flat[i - 1], n, flat_codes[:, b, g : g + n, :], flat_planes[:, b, g : g + n, :])
 
-        def pack_h(h_sorted, g):
-            sources = [h_sorted[:, b, :].bitcast(F32).rearrange("q (u p) -> q u p", u=2) for b in range(BATCH)]
-            grouped = regroup(turn(sources), BATCH, nc.vector.tensor_copy)
-            quantise(grouped, BATCH, h_codes[:, g], h_planes[:, g])
+        def turn_h(h_sorted):
+            return turn([h_sorted[:, b, :].bitcast(F32).rearrange("q (u p) -> q u p", u=2) for b in range(BATCH)])
 
-        h_tiles = []
-        for j in range(N_TILES):
-            h_sorted = work.tile([P, BATCH, K_PASS], BF16, name="h_sorted")
-            h_tiles.append(h_sorted)
-            for b in range(BATCH):
-                acc = banks.tile([P, N_TILE], F32, name="acc", tag="bank")
-                mx_group(
-                    acc[:],
-                    lambda g: flat_codes[:, b, g, :],
-                    lambda g: flat_planes[:, b, g, :],
-                    0,
-                    slice(j * N_TILE, (j + 1) * N_TILE),
-                )
-                nc.scalar.activation(
-                    out=h_sorted[:, b, :].rearrange("q (u p e) -> q u p e", u=2, e=2),
-                    in_=acc[:].rearrange("q (p u e) -> q u p e", u=2, e=2),
-                    func=ACT.Relu,
-                )
-                if b == 0 and j > 0:
-                    pack_h(h_tiles[j - 1], j - 1)
-        pack_h(h_tiles[N_TILES - 1], N_TILES - 1)
+        def quantise_h(turned, g):
+            quantise(regroup(turned, BATCH, nc.vector.tensor_copy), BATCH, h_codes[:, g], h_planes[:, g])
+
+        def relu(h_sorted, acc, b):
+            sorted_out = h_sorted[:, b, :].rearrange("q (u p e) -> q u p e", u=2, e=2)
+            sums = acc[:].rearrange("q (p u e) -> q u p e", u=2, e=2)
+            if b == 0:
+                nc.scalar.activation(out=sorted_out, in_=sums, func=ACT.Relu)
+            else:
+                nc.vector.tensor_scalar_max(out=sorted_out, in0=sums, scalar1=0.0)
+
+        h_sorted = keep.tile([P, N_TILES, BATCH, K_PASS], BF16)
+        h_tiles = [h_sorted[:, j] for j in range(N_TILES)]
+        done = ()
+        for tiles in W1_CHUNKS:
+            accs = {}
+            for j in tiles:
+                for b in range(BATCH):
+                    acc = banks.tile([P, N_TILE], F32, name="acc", tag="bank")
+                    accs[j, b] = acc
+            for g in range(PASSES):
+                for j in tiles:
+                    for b in range(BATCH):
+                        mx_passes(
+                            accs[j, b][:],
+                            lambda g: flat_codes[:, b, g, :],
+                            lambda g: flat_planes[:, b, g, :],
+                            0,
+                            slice(j * N_TILE, (j + 1) * N_TILE),
+                            (g,),
+                        )
+                if g == 1:
+                    turned_h = [turn_h(h_tiles[j]) for j in done]
+                    for j, turned in zip(done, turned_h):
+                        quantise_h(turned, j)
+            for j in tiles:
+                for b in range(BATCH):
+                    relu(h_tiles[j], accs[j, b], b)
+            done = tiles
 
         den = keep.tile([P, BATCH, CH], F32)
         num = keep.tile([P, BATCH, CH], F32)
+        def open_unit(k):
+            wide = banks.tile([P, N_TILE], F32, name="wide", tag="bank")
+            narrow = banks.tile([P, N_TILE], F32, name="narrow", tag="bank")
+            first = k * SUPER
+            return (wide[:], slice(first, first + N_TILE)), (narrow[:, 0:REST], slice(first + N_TILE, first + SUPER))
+
+        def a_passes(part, b, groups=range(PASSES)):
+            acc, cols = part
+            mx_passes(acc, lambda g: h_codes[:, g, b, :], lambda g: h_planes[:, g, b, :], 1, cols, groups)
+
+        early = [open_unit(0) for b in range(BATCH)]
+        a_passes(early[0][0], 0, range(0, 3))
+        last_turned = turn_h(h_tiles[N_TILES - 1])
+        a_passes(early[0][0], 0, range(3, 4))
+        a_passes(early[1][0], 1, range(0, 4))
+        quantise_h(last_turned, N_TILES - 1)
+        for b in range(BATCH):
+            a_passes(early[b][0], b, range(4, 5))
+            a_passes(early[b][1], b)
+
         for k in range(SUPERS):
             first = k * SUPER
             chans = slice(k * P, (k + 1) * P)
             for b in range(BATCH):
-                wide = banks.tile([P, N_TILE], F32, name="wide", tag="bank")
-                narrow = banks.tile([P, N_TILE], F32, name="narrow", tag="bank")
-                for acc, cols in (
-                    (wide[:], slice(first, first + N_TILE)),
-                    (narrow[:, 0:REST], slice(first + N_TILE, first + SUPER)),
-                ):
-                    mx_group(acc, lambda g: h_codes[:, g, b, :], lambda g: h_planes[:, g, b, :], 1, cols)
+                unit = early[b] if k == 0 else open_unit(k)
+                if k > 0:
+                    for part in unit:
+                        a_passes(part, b)
+                wide, narrow = unit[0][0], unit[1][0]
                 th = gate.tile([P, SUPER], F32, name="th")
                 e = gate.tile([P, SUPER], F32, name="e")
                 xe = gate.tile([P, SUPER], F32, name="xe")
-                nc.scalar.activation(out=th[:, 0:N_TILE], in_=wide[:], func=ACT.Tanh, scale=0.5)
-                nc.scalar.activation(out=th[:, N_TILE:SUPER], in_=narrow[:, 0:REST], func=ACT.Tanh, scale=0.5)
+                nc.scalar.activation(out=th[:, 0:N_TILE], in_=wide, func=ACT.Tanh, scale=0.5)
+                nc.scalar.activation(out=th[:, N_TILE:SUPER], in_=narrow, func=ACT.Tanh, scale=0.5)
                 nc.scalar.activation(out=e[:], in_=th[:], func=ACT.Exp, scale=0.5)
                 nc.gpsimd.tensor_tensor(out=xe[:], in0=e[:], in1=flat[:, b, first : first + SUPER], op=ALU.mult)
                 nc.vector.tensor_reduce(

@@ -44,6 +44,7 @@ def tile_dwamformer_pa_kernel(tc, x, w1_words, w1_scales, w2_words, w2_scales, o
 
         ident = keep.tile([P, P], F32)
         warm = keep.tile([P, 2], F32)
+        zeros = keep.tile([P, N_TILE], BF16)
         x_raw = keep.tile([P, BATCH, WIN, CH], BF16)
         flat = keep.tile([P, BATCH, D], BF16)
         flat_cm = flat[:].rearrange("p b (c m) -> p b c m", m=WIN)
@@ -61,6 +62,7 @@ def tile_dwamformer_pa_kernel(tc, x, w1_words, w1_scales, w2_words, w2_scales, o
                 return w_planes[4 * g : P, 2 * which, cols]
             return w_planes[:, 2 * which + 1, cols]
 
+        nc.vector.memset(zeros[:], 0.0)
         nc.vector.memset(warm[:], 0.0)
         nc.vector.memset(w_planes[:, 0:2].rearrange("p s n -> p (s n)").bitcast(I32), 0)
         nc.scalar.activation(out=warm[:, 1:2], in_=warm[:, 0:1], func=ACT.Tanh)
@@ -143,8 +145,19 @@ def tile_dwamformer_pa_kernel(tc, x, w1_words, w1_scales, w2_words, w2_scales, o
             words = flat[:, b, g * K_PASS : (g + 1) * K_PASS].bitcast(F32)
             return words.rearrange("q (p u) -> q u p", u=2)
 
+        idle_bank = banks.tile([P, N_TILE], F32, name="idle_bank", tag="bank")
+
+        def keep_warm(n):
+            for i in range(n):
+                nc.tensor.matmul(idle_bank[:], lhsT=zeros[:, 0:P], rhs=zeros[:], start=True, stop=True)
+
         packs = [(b, g, min(2, PASSES - g)) for b in range(BATCH) for g in range(0, PASSES, 2)]
-        turned_flat = [turn([flat_words(b, g + s) for s in range(n)]) for b, g, n in packs]
+        turned_flat = []
+        keep_warm(8)
+        for b, g, n in packs:
+            turned_flat.append(turn([flat_words(b, g + s) for s in range(n)]))
+            if g + n == PASSES:
+                keep_warm(2)
         grouped_flat = []
         for i in range(len(packs) + 1):
             if i < len(packs):

@@ -25,10 +25,11 @@ N_TILE = 512
 N_TILES = D // N_TILE
 SORT_RUN = 4
 SORT_CUTS = (0, 104, 208, 308, 412, 512)
-SUPER = P * WIN
-SUPERS = D // SUPER
+SECTION_EDGES = (0, 256, 512, 1024, 1536, 2048, 2304, 2560)
+SECTIONS = [slice(lo, hi) for lo, hi in zip(SECTION_EDGES[:-1], SECTION_EDGES[1:])]
+END = len(SECTIONS) - 1
+W2_EDGES = (0, 512, 1024, 1536, 2048, 2304, 2560)
 W1_CHUNKS = ((0, 1), (2, 3), (4,))
-REST = SUPER - N_TILE
 
 FLOPS = 2 * 2 * TOK * D * D
 
@@ -38,7 +39,6 @@ def tile_dwamformer_pa_kernel(tc, x, w1_words, w1_scales, w2_words, w2_scales, o
     with ExitStack() as ctx:
         keep = ctx.enter_context(tc.tile_pool(name="keep", bufs=1))
         work = ctx.enter_context(tc.tile_pool(name="work", bufs=3))
-        gate = ctx.enter_context(tc.tile_pool(name="gate", bufs=4))
         banks = ctx.enter_context(tc.psum_pool(name="banks", bufs=8))
         ctx.enter_context(tc.manual_schedule())
 
@@ -54,8 +54,8 @@ def tile_dwamformer_pa_kernel(tc, x, w1_words, w1_scales, w2_words, w2_scales, o
         w_planes = keep.tile([P, 4, D], U8, align_bytes=64)
         flat_codes = keep.tile([P, BATCH, PASSES, P], U32, align_bytes=64)
         flat_planes = keep.tile([P, BATCH, PASSES, P], U8, align_bytes=64)
-        h_codes = keep.tile([P, PASSES, BATCH, P], U32, align_bytes=64)
-        h_planes = keep.tile([P, PASSES, BATCH, P], U8, align_bytes=64)
+        h_codes = keep.tile([P, BATCH, PASSES, P], U32, align_bytes=64)
+        h_planes = keep.tile([P, BATCH, PASSES, P], U8, align_bytes=64)
 
         def weight_plane(which, g, cols):
             if g < 4:
@@ -84,7 +84,7 @@ def tile_dwamformer_pa_kernel(tc, x, w1_words, w1_scales, w2_words, w2_scales, o
         for b in range(BATCH):
             nc.sync.dma_start(out=x_raw[:, b], in_=x[b].rearrange("(w m) c -> w m c", m=WIN))
         w1_chunks = [slice(tiles[0] * N_TILE, (tiles[-1] + 1) * N_TILE) for tiles in W1_CHUNKS]
-        w2_chunks = [slice(k * SUPER, (k + 1) * SUPER) for k in range(SUPERS)]
+        w2_chunks = [slice(lo, hi) for lo, hi in zip(W2_EDGES[:-1], W2_EDGES[1:])]
         for which, words, scales, chunks in ((0, w1_words, w1_scales, w1_chunks), (1, w2_words, w2_scales, w2_chunks)):
             load_planes(nc.sync, I32, which, scales)
             for cols in chunks:
@@ -167,100 +167,170 @@ def tile_dwamformer_pa_kernel(tc, x, w1_words, w1_scales, w2_words, w2_scales, o
                 b, g, n = packs[i - 1]
                 quantise(grouped_flat[i - 1], n, flat_codes[:, b, g : g + n, :], flat_planes[:, b, g : g + n, :])
 
-        def turn_h(h_sorted):
-            return turn([h_sorted[:, b, :].bitcast(F32).rearrange("q (u p) -> q u p", u=2) for b in range(BATCH)])
+        h_sorted = keep.tile([P, BATCH, N_TILES, K_PASS], BF16)
 
-        def quantise_h(turned, g):
-            quantise(regroup(turned, BATCH, nc.vector.tensor_copy), BATCH, h_codes[:, g], h_planes[:, g])
-
-        def relu(h_sorted, acc, b):
-            sorted_out = h_sorted[:, b, :].rearrange("q (u p e) -> q u p e", u=2, e=2)
-            sums = acc[:].rearrange("q (p u e) -> q u p e", u=2, e=2)
-            if b == 0:
+        def relu(copy_engine, b, j):
+            sorted_out = h_sorted[:, b, j, :].rearrange("q (u p e) -> q u p e", u=2, e=2)
+            sums = h_accs[b, j][:].rearrange("q (p u e) -> q u p e", u=2, e=2)
+            if copy_engine is nc.scalar:
                 nc.scalar.activation(out=sorted_out, in_=sums, func=ACT.Relu)
             else:
                 nc.vector.tensor_scalar_max(out=sorted_out, in0=sums, scalar1=0.0)
 
-        h_sorted = keep.tile([P, N_TILES, BATCH, K_PASS], BF16)
-        h_tiles = [h_sorted[:, j] for j in range(N_TILES)]
-        done = ()
-        for tiles in W1_CHUNKS:
-            accs = {}
-            for j in tiles:
-                for b in range(BATCH):
-                    acc = banks.tile([P, N_TILE], F32, name="acc", tag="bank")
-                    accs[j, b] = acc
-            for g in range(PASSES):
+        def turn_h(b, tiles):
+            return turn([h_sorted[:, b, j, :].bitcast(F32).rearrange("q (u p) -> q u p", u=2) for j in tiles])
+
+        def quantise_h(grouped, b, tiles):
+            groups = slice(tiles[0], tiles[-1] + 1)
+            quantise(grouped, len(tiles), h_codes[:, b, groups, :], h_planes[:, b, groups, :])
+
+        h_accs = {}
+
+        def open_h(tiles, entries):
+            for b in entries:
                 for j in tiles:
-                    for b in range(BATCH):
+                    acc = banks.tile([P, N_TILE], F32, name="acc", tag="bank")
+                    h_accs[b, j] = acc
+
+        def h_passes(tiles, entries, groups):
+            for g in groups:
+                for b in entries:
+                    for j in tiles:
                         mx_passes(
-                            accs[j, b][:],
+                            h_accs[b, j][:],
                             lambda g: flat_codes[:, b, g, :],
                             lambda g: flat_planes[:, b, g, :],
                             0,
                             slice(j * N_TILE, (j + 1) * N_TILE),
                             (g,),
                         )
-                if g == 1:
-                    turned_h = [turn_h(h_tiles[j]) for j in done]
-                    for j, turned in zip(done, turned_h):
-                        quantise_h(turned, j)
-            for j in tiles:
-                for b in range(BATCH):
-                    relu(h_tiles[j], accs[j, b], b)
-            done = tiles
 
+        first, second, last = W1_CHUNKS
+        both = range(BATCH)
+        open_h(first, both)
+        h_passes(first, both, range(PASSES))
+        for j in first:
+            relu(nc.scalar, 0, j)
+            relu(nc.vector, 1, j)
+
+        open_h(second, both)
+        h_passes(second, both, range(0, 2))
+        turned_first = [turn_h(b, first) for b in both]
+        h_passes(second, both, range(2, PASSES))
+        for b in both:
+            quantise_h(regroup(turned_first[b], 2, nc.vector.tensor_copy), b, first)
+        for j in second:
+            relu(nc.scalar, 0, j)
+            relu(nc.vector, 1, j)
+
+        open_h(last, (0,))
+        h_passes(last, (0,), range(PASSES))
+        relu(nc.scalar, 0, last[0])
+        open_h(last, (1,))
+        h_passes(last, (1,), range(0, 3))
+        turned_second = [turn_h(b, second) for b in both]
+        turned_last = turn_h(0, last)
+        h_passes(last, (1,), range(3, PASSES))
+        grouped_second = [regroup(turned_second[0], 2, nc.vector.tensor_copy)]
+        grouped_second.append(regroup(turned_second[1], 2, nc.scalar.copy))
+        quantise_h(grouped_second[0], 0, second)
+        grouped_last = regroup(turned_last, 1, nc.vector.tensor_copy)
+        relu(nc.scalar, 1, last[0])
+        quantise_h(grouped_second[1], 1, second)
+        quantise_h(grouped_last, 0, last)
+
+        e = keep.tile([P, BATCH, D], F32)
+        xe = keep.tile([P, BATCH, D], F32)
         den = keep.tile([P, BATCH, CH], F32)
         num = keep.tile([P, BATCH, CH], F32)
-        def open_unit(k):
-            wide = banks.tile([P, N_TILE], F32, name="wide", tag="bank")
-            narrow = banks.tile([P, N_TILE], F32, name="narrow", tag="bank")
-            first = k * SUPER
-            return (wide[:], slice(first, first + N_TILE)), (narrow[:, 0:REST], slice(first + N_TILE, first + SUPER))
+        a_accs = {}
 
-        def a_passes(part, b, groups=range(PASSES)):
-            acc, cols = part
-            mx_passes(acc, lambda g: h_codes[:, g, b, :], lambda g: h_planes[:, g, b, :], 1, cols, groups)
+        def open_a(s, b):
+            acc = banks.tile([P, N_TILE], F32, name="acc2", tag="bank")
+            a_accs[s, b] = acc[:, 0 : SECTIONS[s].stop - SECTIONS[s].start]
 
-        early = [open_unit(0) for b in range(BATCH)]
-        a_passes(early[0][0], 0, range(0, 3))
-        last_turned = turn_h(h_tiles[N_TILES - 1])
-        a_passes(early[0][0], 0, range(3, 4))
-        a_passes(early[1][0], 1, range(0, 4))
-        quantise_h(last_turned, N_TILES - 1)
-        for b in range(BATCH):
-            a_passes(early[b][0], b, range(4, 5))
-            a_passes(early[b][1], b)
+        def a_passes(s, b, groups=range(PASSES)):
+            mx_passes(
+                a_accs[s, b],
+                lambda g: h_codes[:, b, g, :],
+                lambda g: h_planes[:, b, g, :],
+                1,
+                SECTIONS[s],
+                groups,
+            )
 
-        for k in range(SUPERS):
-            first = k * SUPER
-            chans = slice(k * P, (k + 1) * P)
-            for b in range(BATCH):
-                unit = early[b] if k == 0 else open_unit(k)
-                if k > 0:
-                    for part in unit:
-                        a_passes(part, b)
-                wide, narrow = unit[0][0], unit[1][0]
-                th = gate.tile([P, SUPER], F32, name="th")
-                e = gate.tile([P, SUPER], F32, name="e")
-                xe = gate.tile([P, SUPER], F32, name="xe")
-                nc.scalar.activation(out=th[:, 0:N_TILE], in_=wide, func=ACT.Tanh, scale=0.5)
-                nc.scalar.activation(out=th[:, N_TILE:SUPER], in_=narrow, func=ACT.Tanh, scale=0.5)
-                nc.scalar.activation(out=e[:], in_=th[:], func=ACT.Exp, scale=0.5)
-                nc.gpsimd.tensor_tensor(out=xe[:], in0=e[:], in1=flat[:, b, first : first + SUPER], op=ALU.mult)
-                nc.vector.tensor_reduce(
-                    out=den[:, b, chans], in_=e[:].rearrange("p (c m) -> p c m", m=WIN), axis=AXIS.X, op=ALU.add
-                )
-                nc.vector.tensor_reduce(
-                    out=num[:, b, chans], in_=xe[:].rearrange("p (c m) -> p c m", m=WIN), axis=AXIS.X, op=ALU.add
-                )
+        def halves(s, cut):
+            width = SECTIONS[s].stop - SECTIONS[s].start
+            return (slice(0, width // 2), slice(width // 2, width)) if cut else (slice(0, width),)
 
-        ln_den = keep.tile([P, BATCH, CH], F32)
-        r_den = keep.tile([P, BATCH, CH], F32)
+        def gate_tanh(s, b, part):
+            cols = slice(SECTIONS[s].start + part.start, SECTIONS[s].start + part.stop)
+            nc.scalar.activation(out=e[:, b, cols], in_=a_accs[s, b][:, part], func=ACT.Tanh, scale=0.5)
+
+        def gate_exp(s, b, part):
+            cols = slice(SECTIONS[s].start + part.start, SECTIONS[s].start + part.stop)
+            nc.scalar.activation(out=e[:, b, cols], in_=e[:, b, cols], func=ACT.Exp, scale=0.5)
+
+        def weigh(s, b):
+            engine = nc.vector if s == END else nc.gpsimd
+            cols = SECTIONS[s]
+            engine.tensor_tensor(out=xe[:, b, cols], in0=e[:, b, cols], in1=flat[:, b, cols], op=ALU.mult)
+
+        def sum_windows(sums, values, s, b):
+            chans = slice(SECTIONS[s].start // WIN, SECTIONS[s].stop // WIN)
+            per_frame = values[:, b, chans.start * WIN : chans.stop * WIN].rearrange("p (c m) -> p c m", m=WIN)
+            nc.vector.tensor_reduce(out=sums[:, b, chans], in_=per_frame, axis=AXIS.X, op=ALU.add)
+
+        for s, b in ((0, 0), (1, 0), (0, 1), (1, 1)):
+            open_a(s, b)
+        a_passes(0, 0)
+        a_passes(1, 0)
+        turned_last = turn_h(1, last)
+        a_passes(0, 1, range(0, 4))
+        a_passes(1, 1, range(0, 4))
+        quantise_h(regroup(turned_last, 1, nc.vector.tensor_copy), 1, last)
+        a_passes(0, 1, range(4, PASSES))
+        a_passes(1, 1, range(4, PASSES))
+        units = [(0, 0), (1, 0), (0, 1), (1, 1)] + [(s, b) for s in range(2, END + 1) for b in both]
+
+        steps = [[unit] for unit in units[: 2 * (END - 1)]] + [[(s, b) for b in both] for s in (END - 1, END)]
+        weighed = []
+        for i in range(len(steps)):
+            step = steps[i]
+            if i >= 4:
+                for s, b in step:
+                    open_a(s, b)
+                if step[0][0] < END:
+                    for s, b in step:
+                        a_passes(s, b)
+                else:
+                    for g in range(PASSES):
+                        for s, b in step:
+                            a_passes(s, b, (g,))
+            parts = [(s, b, part) for s, b in step for part in halves(s, i >= 4 and len(step) == 1)]
+            for s, b, part in parts:
+                gate_tanh(s, b, part)
+            for s, b, part in parts:
+                gate_exp(s, b, part)
+            for s, b in step:
+                weigh(s, b)
+            for s, b in step:
+                sum_windows(den, e, s, b)
+                weighed.append((s, b))
+                if len(weighed) > 1:
+                    sum_windows(num, xe, *weighed.pop(0))
+        sum_windows(num, xe, *weighed.pop(0))
+
+        rsqrt = keep.tile([P, BATCH, CH], F32)
+        square = keep.tile([P, CH], F32)
         pooled = keep.tile([P, BATCH, CH], F32)
-        for b in range(BATCH):
-            nc.scalar.activation(out=ln_den[:, b, :], in_=den[:, b, :], func=ACT.Abs_reciprocal_sqrt)
-        for b in range(BATCH):
-            nc.scalar.activation(out=r_den[:, b, :], in_=ln_den[:, b, :], func=ACT.Square)
-            nc.vector.tensor_tensor(out=pooled[:, b, :], in0=num[:, b, :], in1=r_den[:, b, :], op=ALU.mult)
-            nc.sync.dma_start(out=out[b], in_=pooled[:, b, :])
+        for b in both:
+            nc.scalar.activation(out=rsqrt[:, b, :], in_=den[:, b, :], func=ACT.Abs_reciprocal_sqrt)
+        nc.scalar.activation(out=square[:], in_=rsqrt[:, 1, :], func=ACT.Square)
+        for half in (slice(0, CH // 2), slice(CH // 2, CH)):
+            nc.vector.tensor_tensor(out=pooled[:, 0, half], in0=num[:, 0, half], in1=rsqrt[:, 0, half], op=ALU.mult)
+        for half in (slice(0, CH // 2), slice(CH // 2, CH)):
+            nc.vector.tensor_tensor(out=pooled[:, 0, half], in0=pooled[:, 0, half], in1=rsqrt[:, 0, half], op=ALU.mult)
+        nc.sync.dma_start(out=out[0], in_=pooled[:, 0, :])
+        nc.vector.tensor_tensor(out=pooled[:, 1, :], in0=num[:, 1, :], in1=square[:], op=ALU.mult)
+        nc.sync.dma_start(out=out[1], in_=pooled[:, 1, :])

@@ -62,37 +62,50 @@ def tile_dwamformer_pa_kernel(tc, x, w1_words, w1_scales, w2_words, w2_scales, o
                 return w_planes[4 * g : P, 2 * which, cols]
             return w_planes[:, 2 * which + 1, cols]
 
-        nc.vector.memset(zeros[:], 0.0)
+        nc.gpsimd.memset(zeros[:], 0.0)
         nc.vector.memset(warm[:], 0.0)
         nc.vector.memset(w_planes[:, 0:2].rearrange("p s n -> p (s n)").bitcast(I32), 0)
         nc.scalar.activation(out=warm[:, 1:2], in_=warm[:, 0:1], func=ACT.Tanh)
         make_identity(nc, ident[:])
         nc.gpsimd.memset(w_planes[:, 2:4].rearrange("p s n -> p (s n)").bitcast(I32), 0)
 
-        def load_planes(queue, view, which, scales):
+        def load_packed_planes(which, scales):
             for quad in range(4):
-                rows = slice(4 * quad, 4 * quad + 4)
-                queue.dma_start(
-                    out=w_planes[32 * quad : 32 * quad + 16, 2 * which, :].bitcast(view),
-                    in_=scales[0:4, rows, :].bitcast(view),
+                nc.sync.dma_start(
+                    out=w_planes[32 * quad : 32 * quad + 16, 2 * which, :].bitcast(I32),
+                    in_=scales[0:4, 4 * quad : 4 * quad + 4, :].bitcast(I32),
                 )
-                queue.dma_start(
-                    out=w_planes[32 * quad : 32 * quad + 4, 2 * which + 1, :].bitcast(view),
-                    in_=scales[4, rows, :].bitcast(view),
+
+        def load_last_plane(which, scales):
+            for row in range(4):
+                nc.sync.dma_start(
+                    out=w_planes[row:P:32, 2 * which + 1, :].bitcast(I32),
+                    in_=scales[4, row:16:4, :].bitcast(I32),
                 )
+
+        def load_words(which, words, g, cols):
+            nc.sync.dma_start(
+                out=w_sb[which][:, g, cols].bitcast(I32),
+                in_=words[g, :, cols, :].rearrange("p n t -> p (n t)").bitcast(I32),
+            )
 
         for b in range(BATCH):
             nc.sync.dma_start(out=x_raw[:, b], in_=x[b].rearrange("(w m) c -> w m c", m=WIN))
         w1_chunks = [slice(tiles[0] * N_TILE, (tiles[-1] + 1) * N_TILE) for tiles in W1_CHUNKS]
         w2_chunks = [slice(lo, hi) for lo, hi in zip(W2_EDGES[:-1], W2_EDGES[1:])]
-        for which, words, scales, chunks in ((0, w1_words, w1_scales, w1_chunks), (1, w2_words, w2_scales, w2_chunks)):
-            load_planes(nc.sync, I32, which, scales)
-            for cols in chunks:
-                for g in range(PASSES):
-                    nc.sync.dma_start(
-                        out=w_sb[which][:, g, cols].bitcast(I32),
-                        in_=words[g, :, cols, :].rearrange("p n t -> p (n t)").bitcast(I32),
-                    )
+        load_packed_planes(0, w1_scales)
+        for g in range(PASSES - 1):
+            load_words(0, w1_words, g, w1_chunks[0])
+        load_last_plane(0, w1_scales)
+        load_words(0, w1_words, PASSES - 1, w1_chunks[0])
+        for cols in w1_chunks[1:]:
+            for g in range(PASSES):
+                load_words(0, w1_words, g, cols)
+        load_packed_planes(1, w2_scales)
+        load_last_plane(1, w2_scales)
+        for cols in w2_chunks:
+            for g in range(PASSES):
+                load_words(1, w2_words, g, cols)
 
         def turn(sources):
             turned = banks.tile([P, 2, 2, P], F32, name="turned", tag="bank")
@@ -324,13 +337,17 @@ def tile_dwamformer_pa_kernel(tc, x, w1_words, w1_scales, w2_words, w2_scales, o
         rsqrt = keep.tile([P, BATCH, CH], F32)
         square = keep.tile([P, CH], F32)
         pooled = keep.tile([P, BATCH, CH], F32)
+        channel_halves = (slice(0, CH // 2), slice(CH // 2, CH))
         for b in both:
-            nc.scalar.activation(out=rsqrt[:, b, :], in_=den[:, b, :], func=ACT.Abs_reciprocal_sqrt)
-        nc.scalar.activation(out=square[:], in_=rsqrt[:, 1, :], func=ACT.Square)
-        for half in (slice(0, CH // 2), slice(CH // 2, CH)):
+            for half in channel_halves:
+                nc.scalar.activation(out=rsqrt[:, b, half], in_=den[:, b, half], func=ACT.Abs_reciprocal_sqrt)
+        for half in channel_halves:
+            nc.scalar.activation(out=square[:, half], in_=rsqrt[:, 1, half], func=ACT.Square)
+        for half in channel_halves:
             nc.vector.tensor_tensor(out=pooled[:, 0, half], in0=num[:, 0, half], in1=rsqrt[:, 0, half], op=ALU.mult)
-        for half in (slice(0, CH // 2), slice(CH // 2, CH)):
+        for half in channel_halves:
             nc.vector.tensor_tensor(out=pooled[:, 0, half], in0=pooled[:, 0, half], in1=rsqrt[:, 0, half], op=ALU.mult)
         nc.sync.dma_start(out=out[0], in_=pooled[:, 0, :])
-        nc.vector.tensor_tensor(out=pooled[:, 1, :], in0=num[:, 1, :], in1=square[:], op=ALU.mult)
+        for half in channel_halves:
+            nc.vector.tensor_tensor(out=pooled[:, 1, half], in0=num[:, 1, half], in1=square[:, half], op=ALU.mult)
         nc.sync.dma_start(out=out[1], in_=pooled[:, 1, :])

@@ -29,6 +29,7 @@ SECTION_EDGES = (0, 256, 512, 1024, 1536, 2048, 2304, 2560)
 SECTIONS = [slice(lo, hi) for lo, hi in zip(SECTION_EDGES[:-1], SECTION_EDGES[1:])]
 END = len(SECTIONS) - 1
 W2_EDGES = (0, 512, 1024, 1536, 2048, 2304, 2560)
+W1_EDGES = (0, 1024, 2048, 2560)
 W1_CHUNKS = ((0, 1), (2, 3), (4,))
 
 FLOPS = 2 * 2 * TOK * D * D
@@ -48,64 +49,79 @@ def tile_dwamformer_pa_kernel(tc, x, w1_words, w1_scales, w2_words, w2_scales, o
         x_raw = keep.tile([P, BATCH, WIN, CH], BF16)
         flat = keep.tile([P, BATCH, D], BF16)
         flat_cm = flat[:].rearrange("p b (c m) -> p b c m", m=WIN)
-        w1_sb = keep.tile([P, PASSES, D], U32, align_bytes=64)
-        w2_sb = keep.tile([P, PASSES, D], U32, align_bytes=64)
-        w_sb = (w1_sb, w2_sb)
-        w_planes = keep.tile([P, 4, D], U8, align_bytes=64)
+        w_chunks = ([], [])
+        for which, edges in ((0, W1_EDGES), (1, W2_EDGES)):
+            for lo, hi in zip(edges[:-1], edges[1:]):
+                words_sb = keep.tile([P, PASSES, hi - lo], U32, align_bytes=64, name="w%d_from_%d" % (which + 1, lo))
+                w_chunks[which].append((lo, hi, words_sb))
+        w1_packed = keep.tile([P, D], U8, align_bytes=64)
+        w1_last = keep.tile([P, D], U8, align_bytes=64)
+        w2_packed = keep.tile([P, D], U8, align_bytes=64)
+        w2_last = keep.tile([P, D], U8, align_bytes=64)
+        packed_planes = (w1_packed, w2_packed)
+        last_plane = (w1_last, w2_last)
         flat_codes = keep.tile([P, BATCH, PASSES, P], U32, align_bytes=64)
         flat_planes = keep.tile([P, BATCH, PASSES, P], U8, align_bytes=64)
         h_codes = keep.tile([P, BATCH, PASSES, P], U32, align_bytes=64)
         h_planes = keep.tile([P, BATCH, PASSES, P], U8, align_bytes=64)
 
+        def weight_words(which, g, cols):
+            for lo, hi, words_sb in w_chunks[which]:
+                if lo <= cols.start < hi:
+                    return words_sb[:, g, cols.start - lo : cols.stop - lo]
+
         def weight_plane(which, g, cols):
             if g < 4:
-                return w_planes[4 * g : P, 2 * which, cols]
-            return w_planes[:, 2 * which + 1, cols]
+                return packed_planes[which][4 * g : P, cols]
+            return last_plane[which][:, cols]
 
         nc.gpsimd.memset(zeros[:], 0.0)
         nc.vector.memset(warm[:], 0.0)
-        nc.vector.memset(w_planes[:, 0:2].rearrange("p s n -> p (s n)").bitcast(I32), 0)
+        nc.vector.memset(w1_packed[:].bitcast(I32), 0)
+        nc.vector.memset(w1_last[:].bitcast(I32), 0)
         nc.scalar.activation(out=warm[:, 1:2], in_=warm[:, 0:1], func=ACT.Tanh)
         make_identity(nc, ident[:])
-        nc.gpsimd.memset(w_planes[:, 2:4].rearrange("p s n -> p (s n)").bitcast(I32), 0)
+        nc.gpsimd.memset(w2_packed[:].bitcast(I32), 0)
+        nc.gpsimd.memset(w2_last[:].bitcast(I32), 0)
 
         def load_packed_planes(which, scales):
             for quad in range(4):
                 nc.sync.dma_start(
-                    out=w_planes[32 * quad : 32 * quad + 16, 2 * which, :].bitcast(I32),
+                    out=packed_planes[which][32 * quad : 32 * quad + 16, :].bitcast(I32),
                     in_=scales[0:4, 4 * quad : 4 * quad + 4, :].bitcast(I32),
                 )
 
         def load_last_plane(which, scales):
             for row in range(4):
                 nc.sync.dma_start(
-                    out=w_planes[row:P:32, 2 * which + 1, :].bitcast(I32),
+                    out=last_plane[which][row:P:32, :].bitcast(I32),
                     in_=scales[4, row:16:4, :].bitcast(I32),
                 )
 
-        def load_words(which, words, g, cols):
+        def load_words(which, words, chunk, groups):
+            lo, hi, words_sb = w_chunks[which][chunk]
             nc.sync.dma_start(
-                out=w_sb[which][:, g, cols].bitcast(I32),
-                in_=words[g, :, cols, :].rearrange("p n t -> p (n t)").bitcast(I32),
+                out=words_sb[:, groups, :].bitcast(I32),
+                in_=words[groups, :, lo:hi, :].rearrange("g p n t -> p g (n t)").bitcast(I32),
             )
 
         for b in range(BATCH):
             nc.sync.dma_start(out=x_raw[:, b], in_=x[b].rearrange("(w m) c -> w m c", m=WIN))
-        w1_chunks = [slice(tiles[0] * N_TILE, (tiles[-1] + 1) * N_TILE) for tiles in W1_CHUNKS]
-        w2_chunks = [slice(lo, hi) for lo, hi in zip(W2_EDGES[:-1], W2_EDGES[1:])]
         load_packed_planes(0, w1_scales)
-        for g in range(PASSES - 1):
-            load_words(0, w1_words, g, w1_chunks[0])
+        load_words(0, w1_words, 0, slice(0, 1))
+        load_words(0, w1_words, 0, slice(1, 3))
         load_last_plane(0, w1_scales)
-        load_words(0, w1_words, PASSES - 1, w1_chunks[0])
-        for cols in w1_chunks[1:]:
-            for g in range(PASSES):
-                load_words(0, w1_words, g, cols)
+        load_words(0, w1_words, 0, slice(3, 5))
+        load_words(0, w1_words, 1, slice(0, 2))
+        load_words(0, w1_words, 1, slice(2, 5))
+        load_words(0, w1_words, 2, slice(0, 4))
+        load_words(0, w1_words, 2, slice(4, 5))
         load_packed_planes(1, w2_scales)
         load_last_plane(1, w2_scales)
-        for cols in w2_chunks:
-            for g in range(PASSES):
-                load_words(1, w2_words, g, cols)
+        load_words(1, w2_words, 0, slice(0, 3))
+        load_words(1, w2_words, 0, slice(3, 5))
+        for chunk in range(1, len(w_chunks[1])):
+            load_words(1, w2_words, chunk, slice(0, 5))
 
         def turn(sources):
             turned = banks.tile([P, 2, 2, P], F32, name="turned", tag="bank")
@@ -135,7 +151,7 @@ def tile_dwamformer_pa_kernel(tc, x, w1_words, w1_scales, w2_words, w2_scales, o
                     out=acc,
                     lhsT=codes_of(g).bitcast(FP8X4),
                     lhsT_scale=planes_of(g),
-                    rhs=w_sb[which][:, g, cols].bitcast(FP8X4),
+                    rhs=weight_words(which, g, cols).bitcast(FP8X4),
                     rhs_scale=weight_plane(which, g, cols),
                     start=(g == 0),
                     stop=(g == PASSES - 1),
@@ -166,10 +182,10 @@ def tile_dwamformer_pa_kernel(tc, x, w1_words, w1_scales, w2_words, w2_scales, o
 
         packs = [(b, g, min(2, PASSES - g)) for b in range(BATCH) for g in range(0, PASSES, 2)]
         turned_flat = []
-        keep_warm(8)
+        keep_warm(7)
         for b, g, n in packs:
             turned_flat.append(turn([flat_words(b, g + s) for s in range(n)]))
-            if g + n == PASSES:
+            if (b, g + n) == (0, PASSES):
                 keep_warm(2)
         grouped_flat = []
         for i in range(len(packs) + 1):
@@ -221,7 +237,9 @@ def tile_dwamformer_pa_kernel(tc, x, w1_words, w1_scales, w2_words, w2_scales, o
         first, second, last = W1_CHUNKS
         both = range(BATCH)
         open_h(first, both)
-        h_passes(first, both, range(PASSES))
+        for b in both:
+            h_passes(first, (b,), range(0, 3))
+        h_passes(first, both, range(3, PASSES))
         for j in first:
             relu(nc.scalar, 0, j)
             relu(nc.vector, 1, j)

@@ -25,7 +25,7 @@ N_TILE = 512
 N_TILES = D // N_TILE
 SORT_RUN = 4
 SORT_CUTS = (0, 104, 208, 308, 412, 512)
-SECTION_EDGES = (0, 256, 512, 1024, 1536, 2048, 2304, 2560)
+SECTION_EDGES = (0, 256, 512, 1024, 1536, 2048, 2304, 2432, 2560)
 SECTIONS = [slice(lo, hi) for lo, hi in zip(SECTION_EDGES[:-1], SECTION_EDGES[1:])]
 END = len(SECTIONS) - 1
 W2_EDGES = (0, 512, 1024, 1536, 2048, 2304, 2560)
@@ -109,7 +109,8 @@ def tile_dwamformer_pa_kernel(tc, x, w1_words, w1_scales, w2_words, w2_scales, o
             nc.sync.dma_start(out=x_raw[:, b], in_=x[b].rearrange("(w m) c -> w m c", m=WIN))
         load_packed_planes(0, w1_scales)
         load_words(0, w1_words, 0, slice(0, 1))
-        load_words(0, w1_words, 0, slice(1, 3))
+        load_words(0, w1_words, 0, slice(1, 2))
+        load_words(0, w1_words, 0, slice(2, 3))
         load_last_plane(0, w1_scales)
         load_words(0, w1_words, 0, slice(3, 5))
         load_words(0, w1_words, 1, slice(0, 2))
@@ -238,8 +239,8 @@ def tile_dwamformer_pa_kernel(tc, x, w1_words, w1_scales, w2_words, w2_scales, o
         both = range(BATCH)
         open_h(first, both)
         for b in both:
-            h_passes(first, (b,), range(0, 3))
-        h_passes(first, both, range(3, PASSES))
+            h_passes(first, (b,), range(0, 2))
+        h_passes(first, both, range(2, PASSES))
         for j in first:
             relu(nc.scalar, 0, j)
             relu(nc.vector, 1, j)
@@ -259,16 +260,17 @@ def tile_dwamformer_pa_kernel(tc, x, w1_words, w1_scales, w2_words, w2_scales, o
         relu(nc.scalar, 0, last[0])
         open_h(last, (1,))
         h_passes(last, (1,), range(0, 3))
-        turned_second = [turn_h(b, second) for b in both]
+        turned_second = [turn_h(0, second)]
         turned_last = turn_h(0, last)
+        turned_second.append(turn_h(1, second))
         h_passes(last, (1,), range(3, PASSES))
         grouped_second = [regroup(turned_second[0], 2, nc.vector.tensor_copy)]
-        grouped_second.append(regroup(turned_second[1], 2, nc.scalar.copy))
-        quantise_h(grouped_second[0], 0, second)
         grouped_last = regroup(turned_last, 1, nc.vector.tensor_copy)
+        grouped_second.append(regroup(turned_second[1], 2, nc.scalar.copy))
         relu(nc.scalar, 1, last[0])
-        quantise_h(grouped_second[1], 1, second)
+        quantise_h(grouped_second[0], 0, second)
         quantise_h(grouped_last, 0, last)
+        quantise_h(grouped_second[1], 1, second)
 
         e = keep.tile([P, BATCH, D], F32)
         xe = keep.tile([P, BATCH, D], F32)
@@ -303,7 +305,7 @@ def tile_dwamformer_pa_kernel(tc, x, w1_words, w1_scales, w2_words, w2_scales, o
             nc.scalar.activation(out=e[:, b, cols], in_=e[:, b, cols], func=ACT.Exp, scale=0.5)
 
         def weigh(s, b):
-            engine = nc.vector if s == END else nc.gpsimd
+            engine = nc.vector if (s, b) == (2, 0) or s >= END - 1 else nc.gpsimd
             cols = SECTIONS[s]
             engine.tensor_tensor(out=xe[:, b, cols], in0=e[:, b, cols], in1=flat[:, b, cols], op=ALU.mult)
 

@@ -28,7 +28,7 @@ SORT_CUTS = (0, 104, 208, 308, 412, 512)
 SECTION_EDGES = (0, 256, 512, 1024, 1536, 2048, 2304, 2432, 2560)
 SECTIONS = [slice(lo, hi) for lo, hi in zip(SECTION_EDGES[:-1], SECTION_EDGES[1:])]
 END = len(SECTIONS) - 1
-W2_EDGES = (0, 512, 1024, 1536, 2048, 2304, 2560)
+W2_EDGES = (0, 512, 1024, 1536, 2048, 2304, 2432, 2560)
 W1_EDGES = (0, 1024, 2048, 2560)
 W1_CHUNKS = ((0, 1), (2, 3), (4,))
 
@@ -121,8 +121,10 @@ def tile_dwamformer_pa_kernel(tc, x, w1_words, w1_scales, w2_words, w2_scales, o
         load_last_plane(1, w2_scales)
         load_words(1, w2_words, 0, slice(0, 3))
         load_words(1, w2_words, 0, slice(3, 5))
-        for chunk in range(1, len(w_chunks[1])):
+        for chunk in range(1, len(w_chunks[1]) - 1):
             load_words(1, w2_words, chunk, slice(0, 5))
+        load_words(1, w2_words, len(w_chunks[1]) - 1, slice(0, 4))
+        load_words(1, w2_words, len(w_chunks[1]) - 1, slice(4, 5))
 
         def turn(sources):
             turned = banks.tile([P, 2, 2, P], F32, name="turned", tag="bank")
@@ -305,12 +307,13 @@ def tile_dwamformer_pa_kernel(tc, x, w1_words, w1_scales, w2_words, w2_scales, o
             nc.scalar.activation(out=e[:, b, cols], in_=e[:, b, cols], func=ACT.Exp, scale=0.5)
 
         def weigh(s, b):
-            engine = nc.vector if (s, b) == (2, 0) or s >= END - 1 else nc.gpsimd
+            engine = nc.vector if s in (0, END) else nc.gpsimd
             cols = SECTIONS[s]
             engine.tensor_tensor(out=xe[:, b, cols], in0=e[:, b, cols], in1=flat[:, b, cols], op=ALU.mult)
 
         def sum_windows(sums, values, s, b):
-            chans = slice(SECTIONS[s].start // WIN, SECTIONS[s].stop // WIN)
+            first = END - 1 if s == END else s
+            chans = slice(SECTIONS[first].start // WIN, SECTIONS[s].stop // WIN)
             per_frame = values[:, b, chans.start * WIN : chans.stop * WIN].rearrange("p (c m) -> p c m", m=WIN)
             nc.vector.tensor_reduce(out=sums[:, b, chans], in_=per_frame, axis=AXIS.X, op=ALU.add)
 
@@ -348,8 +351,9 @@ def tile_dwamformer_pa_kernel(tc, x, w1_words, w1_scales, w2_words, w2_scales, o
             for s, b in step:
                 weigh(s, b)
             for s, b in step:
-                sum_windows(den, e, s, b)
-                weighed.append((s, b))
+                if s != END - 1:
+                    sum_windows(den, e, s, b)
+                    weighed.append((s, b))
                 if len(weighed) > 1:
                     sum_windows(num, xe, *weighed.pop(0))
         sum_windows(num, xe, *weighed.pop(0))
@@ -370,4 +374,4 @@ def tile_dwamformer_pa_kernel(tc, x, w1_words, w1_scales, w2_words, w2_scales, o
         nc.sync.dma_start(out=out[0], in_=pooled[:, 0, :])
         for half in channel_halves:
             nc.vector.tensor_tensor(out=pooled[:, 1, half], in0=num[:, 1, half], in1=square[:, half], op=ALU.mult)
-        nc.sync.dma_start(out=out[1], in_=pooled[:, 1, :])
+            nc.sync.dma_start(out=out[1, :, half], in_=pooled[:, 1, half])

from contextlib import ExitStack

import concourse.mybir as mybir
from concourse.masks import make_identity

F32 = mybir.dt.float32
BF16 = mybir.dt.bfloat16
I32 = mybir.dt.int32
U32 = mybir.dt.uint32
U8 = mybir.dt.uint8
FP8X4 = mybir.dt.float8_e4m3fn_x4
ACT = mybir.ActivationFunctionType
ALU = mybir.AluOpType
AXIS = mybir.AxisListType

P = 128
BATCH = 2
WIN = 5
CH = 512
D = CH * WIN
TOK = BATCH * P
K_PASS = 512
PASSES = D // K_PASS
N_TILE = 512
N_TILES = D // N_TILE
SORT_RUN = 4
SORT_CUTS = (0, 104, 208, 308, 412, 512)
SECTION_EDGES = (0, 256, 512, 1024, 1536, 2048, 2304, 2432, 2560)
SECTIONS = [slice(lo, hi) for lo, hi in zip(SECTION_EDGES[:-1], SECTION_EDGES[1:])]
END = len(SECTIONS) - 1
W2_EDGES = (0, 512, 1024, 1536, 2048, 2304, 2432, 2560)
W1_EDGES = (0, 1024, 2048, 2560)
W1_CHUNKS = ((0, 1), (2, 3), (4,))

FLOPS = 2 * 2 * TOK * D * D


def tile_dwamformer_pa_kernel(tc, x, w1_words, w1_scales, w2_words, w2_scales, out):
    nc = tc.nc
    with ExitStack() as ctx:
        keep = ctx.enter_context(tc.tile_pool(name="keep", bufs=1))
        work = ctx.enter_context(tc.tile_pool(name="work", bufs=3))
        banks = ctx.enter_context(tc.psum_pool(name="banks", bufs=8))
        ctx.enter_context(tc.manual_schedule())

        ident = keep.tile([P, P], F32)
        warm = keep.tile([P, 2], F32)
        zeros = keep.tile([P, N_TILE], BF16)
        x_raw = keep.tile([P, BATCH, WIN, CH], BF16)
        flat = keep.tile([P, BATCH, D], BF16)
        flat_cm = flat[:].rearrange("p b (c m) -> p b c m", m=WIN)
        w_chunks = ([], [])
        for which, edges in ((0, W1_EDGES), (1, W2_EDGES)):
            for lo, hi in zip(edges[:-1], edges[1:]):
                words_sb = keep.tile([P, PASSES, hi - lo], U32, align_bytes=64, name="w%d_from_%d" % (which + 1, lo))
                w_chunks[which].append((lo, hi, words_sb))
        w1_packed = keep.tile([P, D], U8, align_bytes=64)
        w1_last = keep.tile([P, D], U8, align_bytes=64)
        w2_packed = keep.tile([P, D], U8, align_bytes=64)
        w2_last = keep.tile([P, D], U8, align_bytes=64)
        packed_planes = (w1_packed, w2_packed)
        last_plane = (w1_last, w2_last)
        flat_codes = keep.tile([P, BATCH, PASSES, P], U32, align_bytes=64)
        flat_planes = keep.tile([P, BATCH, PASSES, P], U8, align_bytes=64)
        h_codes = keep.tile([P, BATCH, PASSES, P], U32, align_bytes=64)
        h_planes = keep.tile([P, BATCH, PASSES, P], U8, align_bytes=64)

        def weight_words(which, g, cols):
            for lo, hi, words_sb in w_chunks[which]:
                if lo <= cols.start < hi:
                    return words_sb[:, g, cols.start - lo : cols.stop - lo]

        def weight_plane(which, g, cols):
            if g < 4:
                return packed_planes[which][4 * g : P, cols]
            return last_plane[which][:, cols]

        nc.gpsimd.memset(zeros[:], 0.0)
        nc.vector.memset(warm[:], 0.0)
        nc.vector.memset(w1_packed[:].bitcast(I32), 0)
        nc.vector.memset(w1_last[:].bitcast(I32), 0)
        nc.scalar.activation(out=warm[:, 1:2], in_=warm[:, 0:1], func=ACT.Tanh)
        make_identity(nc, ident[:])
        nc.gpsimd.memset(w2_packed[:].bitcast(I32), 0)
        nc.gpsimd.memset(w2_last[:].bitcast(I32), 0)

        def load_packed_planes(which, scales):
            for quad in range(4):
                nc.sync.dma_start(
                    out=packed_planes[which][32 * quad : 32 * quad + 16, :].bitcast(I32),
                    in_=scales[0:4, 4 * quad : 4 * quad + 4, :].bitcast(I32),
                )

        def load_last_plane(which, scales):
            for row in range(4):
                nc.sync.dma_start(
                    out=last_plane[which][row:P:32, :].bitcast(I32),
                    in_=scales[4, row:16:4, :].bitcast(I32),
                )

        def load_words(which, words, chunk, groups):
            lo, hi, words_sb = w_chunks[which][chunk]
            nc.sync.dma_start(
                out=words_sb[:, groups, :].bitcast(I32),
                in_=words[groups, :, lo:hi, :].rearrange("g p n t -> p g (n t)").bitcast(I32),
            )

        for b in range(BATCH):
            nc.sync.dma_start(out=x_raw[:, b], in_=x[b].rearrange("(w m) c -> w m c", m=WIN))
        load_packed_planes(0, w1_scales)
        load_words(0, w1_words, 0, slice(0, 1))
        load_words(0, w1_words, 0, slice(1, 2))
        load_words(0, w1_words, 0, slice(2, 3))
        load_last_plane(0, w1_scales)
        load_words(0, w1_words, 0, slice(3, 5))
        load_words(0, w1_words, 1, slice(0, 2))
        load_words(0, w1_words, 1, slice(2, 5))
        load_words(0, w1_words, 2, slice(0, 4))
        load_words(0, w1_words, 2, slice(4, 5))
        load_packed_planes(1, w2_scales)
        load_last_plane(1, w2_scales)
        load_words(1, w2_words, 0, slice(0, 3))
        load_words(1, w2_words, 0, slice(3, 5))
        for chunk in range(1, len(w_chunks[1]) - 1):
            load_words(1, w2_words, chunk, slice(0, 5))
        load_words(1, w2_words, len(w_chunks[1]) - 1, slice(0, 4))
        load_words(1, w2_words, len(w_chunks[1]) - 1, slice(4, 5))

        def turn(sources):
            turned = banks.tile([P, 2, 2, P], F32, name="turned", tag="bank")
            for s in range(len(sources)):
                for u in range(2):
                    nc.tensor.transpose(turned[:, s, u, :], sources[s][:, u, :], ident[:])
            return turned

        def regroup(turned, n, copy):
            grouped = work.tile([P, 2 * K_PASS], BF16, align_bytes=64, name="grouped")
            copy(
                out=grouped[:, 0 : n * K_PASS].bitcast(F32).rearrange("p (s r u) -> p s r u", s=n, u=2),
                in_=turned[:, 0:n].rearrange("p s u r -> p s r u"),
            )
            return grouped

        def quantise(grouped, n, codes, planes):
            nc.vector.quantize_mx(
                out=codes.rearrange("p s r -> p (s r)").bitcast(FP8X4),
                scales=planes.rearrange("p s r -> p (s r)"),
                in_=grouped[:, 0 : n * K_PASS],
            )

        def mx_passes(acc, codes_of, planes_of, which, cols, groups=range(PASSES)):
            for g in groups:
                nc.tensor.matmul_mx(
                    out=acc,
                    lhsT=codes_of(g).bitcast(FP8X4),
                    lhsT_scale=planes_of(g),
                    rhs=weight_words(which, g, cols).bitcast(FP8X4),
                    rhs_scale=weight_plane(which, g, cols),
                    start=(g == 0),
                    stop=(g == PASSES - 1),
                )

        def sort(copy, b, step):
            chans = slice(SORT_CUTS[step], SORT_CUTS[step + 1])
            copy(
                out=flat_cm[:, b, chans, :].rearrange("p (c i) m -> p c m i", i=SORT_RUN),
                in_=x_raw[:, b, :, chans].rearrange("p m (c i) -> p c m i", i=SORT_RUN),
            )

        for b in range(BATCH):
            for step in range(3):
                sort(nc.vector.tensor_copy, b, step)
            for step in range(3, 5):
                sort(nc.scalar.copy, b, step)

        def flat_words(b, g):
            words = flat[:, b, g * K_PASS : (g + 1) * K_PASS].bitcast(F32)
            return words.rearrange("q (p u) -> q u p", u=2)

        idle_bank = banks.tile([P, N_TILE], F32, name="idle_bank", tag="bank")

        def keep_warm(n):
            for i in range(n):
                nc.tensor.matmul(idle_bank[:], lhsT=zeros[:, 0:P], rhs=zeros[:], start=True, stop=True)

        packs = [(b, g, min(2, PASSES - g)) for b in range(BATCH) for g in range(0, PASSES, 2)]
        turned_flat = []
        keep_warm(7)
        for b, g, n in packs:
            turned_flat.append(turn([flat_words(b, g + s) for s in range(n)]))
            if (b, g + n) == (0, PASSES):
                keep_warm(2)
        grouped_flat = []
        for i in range(len(packs) + 1):
            if i < len(packs):
                copy = nc.scalar.copy if i % 2 == 0 else nc.vector.tensor_copy
                grouped_flat.append(regroup(turned_flat[i], packs[i][2], copy))
            if i > 0:
                b, g, n = packs[i - 1]
                quantise(grouped_flat[i - 1], n, flat_codes[:, b, g : g + n, :], flat_planes[:, b, g : g + n, :])

        h_sorted = keep.tile([P, BATCH, N_TILES, K_PASS], BF16)

        def relu(copy_engine, b, j):
            sorted_out = h_sorted[:, b, j, :].rearrange("q (u p e) -> q u p e", u=2, e=2)
            sums = h_accs[b, j][:].rearrange("q (p u e) -> q u p e", u=2, e=2)
            if copy_engine is nc.scalar:
                nc.scalar.activation(out=sorted_out, in_=sums, func=ACT.Relu)
            else:
                nc.vector.tensor_scalar_max(out=sorted_out, in0=sums, scalar1=0.0)

        def turn_h(b, tiles):
            return turn([h_sorted[:, b, j, :].bitcast(F32).rearrange("q (u p) -> q u p", u=2) for j in tiles])

        def quantise_h(grouped, b, tiles):
            groups = slice(tiles[0], tiles[-1] + 1)
            quantise(grouped, len(tiles), h_codes[:, b, groups, :], h_planes[:, b, groups, :])

        h_accs = {}

        def open_h(tiles, entries):
            for b in entries:
                for j in tiles:
                    acc = banks.tile([P, N_TILE], F32, name="acc", tag="bank")
                    h_accs[b, j] = acc

        def h_passes(tiles, entries, groups):
            for g in groups:
                for b in entries:
                    for j in tiles:
                        mx_passes(
                            h_accs[b, j][:],
                            lambda g: flat_codes[:, b, g, :],
                            lambda g: flat_planes[:, b, g, :],
                            0,
                            slice(j * N_TILE, (j + 1) * N_TILE),
                            (g,),
                        )

        first, second, last = W1_CHUNKS
        both = range(BATCH)
        open_h(first, both)
        for b in both:
            h_passes(first, (b,), range(0, 2))
        h_passes(first, both, range(2, PASSES))
        for j in first:
            relu(nc.scalar, 0, j)
            relu(nc.vector, 1, j)

        open_h(second, both)
        h_passes(second, both, range(0, 2))
        turned_first = [turn_h(b, first) for b in both]
        h_passes(second, both, range(2, PASSES))
        for b in both:
            quantise_h(regroup(turned_first[b], 2, nc.vector.tensor_copy), b, first)
        for j in second:
            relu(nc.scalar, 0, j)
            relu(nc.vector, 1, j)

        open_h(last, (0,))
        h_passes(last, (0,), range(PASSES))
        relu(nc.scalar, 0, last[0])
        open_h(last, (1,))
        h_passes(last, (1,), range(0, 3))
        turned_second = [turn_h(0, second)]
        turned_last = turn_h(0, last)
        turned_second.append(turn_h(1, second))
        h_passes(last, (1,), range(3, PASSES))
        grouped_second = [regroup(turned_second[0], 2, nc.vector.tensor_copy)]
        grouped_last = regroup(turned_last, 1, nc.vector.tensor_copy)
        grouped_second.append(regroup(turned_second[1], 2, nc.scalar.copy))
        relu(nc.scalar, 1, last[0])
        quantise_h(grouped_second[0], 0, second)
        quantise_h(grouped_last, 0, last)
        quantise_h(grouped_second[1], 1, second)

        e = keep.tile([P, BATCH, D], F32)
        xe = keep.tile([P, BATCH, D], F32)
        den = keep.tile([P, BATCH, CH], F32)
        num = keep.tile([P, BATCH, CH], F32)
        a_accs = {}

        def open_a(s, b):
            acc = banks.tile([P, N_TILE], F32, name="acc2", tag="bank")
            a_accs[s, b] = acc[:, 0 : SECTIONS[s].stop - SECTIONS[s].start]

        def a_passes(s, b, groups=range(PASSES)):
            mx_passes(
                a_accs[s, b],
                lambda g: h_codes[:, b, g, :],
                lambda g: h_planes[:, b, g, :],
                1,
                SECTIONS[s],
                groups,
            )

        def halves(s, cut):
            width = SECTIONS[s].stop - SECTIONS[s].start
            return (slice(0, width // 2), slice(width // 2, width)) if cut else (slice(0, width),)

        def gate_tanh(s, b, part):
            cols = slice(SECTIONS[s].start + part.start, SECTIONS[s].start + part.stop)
            nc.scalar.activation(out=e[:, b, cols], in_=a_accs[s, b][:, part], func=ACT.Tanh, scale=0.5)

        def gate_exp(s, b, part):
            cols = slice(SECTIONS[s].start + part.start, SECTIONS[s].start + part.stop)
            nc.scalar.activation(out=e[:, b, cols], in_=e[:, b, cols], func=ACT.Exp, scale=0.5)

        def weigh(s, b):
            engine = nc.vector if s in (0, END) else nc.gpsimd
            cols = SECTIONS[s]
            engine.tensor_tensor(out=xe[:, b, cols], in0=e[:, b, cols], in1=flat[:, b, cols], op=ALU.mult)

        def sum_windows(sums, values, s, b):
            first = END - 1 if s == END else s
            chans = slice(SECTIONS[first].start // WIN, SECTIONS[s].stop // WIN)
            per_frame = values[:, b, chans.start * WIN : chans.stop * WIN].rearrange("p (c m) -> p c m", m=WIN)
            nc.vector.tensor_reduce(out=sums[:, b, chans], in_=per_frame, axis=AXIS.X, op=ALU.add)

        for s, b in ((0, 0), (1, 0), (0, 1), (1, 1)):
            open_a(s, b)
        a_passes(0, 0)
        a_passes(1, 0)
        turned_last = turn_h(1, last)
        a_passes(0, 1, range(0, 4))
        a_passes(1, 1, range(0, 4))
        quantise_h(regroup(turned_last, 1, nc.vector.tensor_copy), 1, last)
        a_passes(0, 1, range(4, PASSES))
        a_passes(1, 1, range(4, PASSES))
        units = [(0, 0), (1, 0), (0, 1), (1, 1)] + [(s, b) for s in range(2, END + 1) for b in both]

        steps = [[unit] for unit in units[: 2 * (END - 1)]] + [[(s, b) for b in both] for s in (END - 1, END)]
        weighed = []
        for i in range(len(steps)):
            step = steps[i]
            if i >= 4:
                for s, b in step:
                    open_a(s, b)
                if step[0][0] < END:
                    for s, b in step:
                        a_passes(s, b)
                else:
                    for g in range(PASSES):
                        for s, b in step:
                            a_passes(s, b, (g,))
            parts = [(s, b, part) for s, b in step for part in halves(s, i >= 4 and len(step) == 1)]
            for s, b, part in parts:
                gate_tanh(s, b, part)
            for s, b, part in parts:
                gate_exp(s, b, part)
            for s, b in step:
                weigh(s, b)
            for s, b in step:
                if s != END - 1:
                    sum_windows(den, e, s, b)
                    weighed.append((s, b))
                if len(weighed) > 1:
                    sum_windows(num, xe, *weighed.pop(0))
        sum_windows(num, xe, *weighed.pop(0))

        rsqrt = keep.tile([P, BATCH, CH], F32)
        square = keep.tile([P, CH], F32)
        pooled = keep.tile([P, BATCH, CH], F32)
        channel_halves = (slice(0, CH // 2), slice(CH // 2, CH))
        for b in both:
            for half in channel_halves:
                nc.scalar.activation(out=rsqrt[:, b, half], in_=den[:, b, half], func=ACT.Abs_reciprocal_sqrt)
        for half in channel_halves:
            nc.scalar.activation(out=square[:, half], in_=rsqrt[:, 1, half], func=ACT.Square)
        for half in channel_halves:
            nc.vector.tensor_tensor(out=pooled[:, 0, half], in0=num[:, 0, half], in1=rsqrt[:, 0, half], op=ALU.mult)
        for half in channel_halves:
            nc.vector.tensor_tensor(out=pooled[:, 0, half], in0=pooled[:, 0, half], in1=rsqrt[:, 0, half], op=ALU.mult)
        nc.sync.dma_start(out=out[0], in_=pooled[:, 0, :])
        for half in channel_halves:
            nc.vector.tensor_tensor(out=pooled[:, 1, half], in0=num[:, 1, half], in1=square[:, half], op=ALU.mult)
            nc.sync.dma_start(out=out[1, :, half], in_=pooled[:, 1, half])
